import numpy as np
import ml_dtypes


def mxq(x, axis, fmt="e4m3"):
    dtype, down = {"e4m3": (ml_dtypes.float8_e4m3fn, 7), "e5m2": (ml_dtypes.float8_e5m2, 14)}[fmt]
    v = np.moveaxis(np.asarray(x, np.float32).astype(ml_dtypes.bfloat16).astype(np.float64), axis, -1)
    blocks = v.reshape(v.shape[:-1] + (-1, 32))
    amax = np.abs(blocks).max(-1, keepdims=True)
    byte = np.maximum(np.where(amax > 0, np.frexp(amax)[1] - 1 + 127, 0) - down, 1)
    scale = np.exp2(byte - 127.0)
    codes = (blocks / scale).astype(np.float32).astype(dtype).astype(np.float64)
    return np.moveaxis((codes * scale).reshape(v.shape), -1, axis)


WIDE = False


def mx_kscale(k):
    if not WIDE:
        return np.ones(k)
    levels = np.array([10, -10, 5, -5, 0])
    if k % 512:
        return np.exp2(np.random.permutation(np.resize(levels, k // 32))).repeat(32)
    a = np.empty((k // 512, 16))
    for p in range(k // 512):
        a[p, :8] = np.random.permutation(np.resize(levels, 8))
        for g in range(8):
            far = levels[np.abs(levels - a[p, g]) >= 10]
            a[p, g + 8] = far[np.random.randint(len(far))]
    return np.exp2(a.ravel()).repeat(32)


BF16 = ml_dtypes.bfloat16


def bf(x):
    return np.asarray(x, np.float32).astype(BF16)


def f64(x):
    return np.asarray(x).astype(np.float64)


E2M1 = np.array([0.0, 0.5, 1.0, 1.5, 2.0, 3.0, 4.0, 6.0, -0.0, -0.5, -1.0, -1.5, -2.0, -3.0, -4.0, -6.0])


def pack_weight(w, fmt):
    k, n = w.shape
    w = f64(bf(w)).reshape(k // 32, 32, n)
    amax = np.abs(w).max(1)
    if fmt == "e4m3":
        byte = np.frexp(amax)[1] - 1 + 127 - 7
    else:
        mant, ex = np.frexp(amax / 6.0)
        byte = np.where(mant > 0.5, ex, ex - 1) + 127
    byte = np.clip(np.where(amax > 0, byte, 1), 1, 254)
    scaled = (w * np.exp2(127.0 - byte)[:, None, :]).reshape(k, n).astype(np.float32)
    by_word = np.ascontiguousarray(scaled.reshape(k // 512, 128, 4, n).transpose(0, 1, 3, 2))
    if fmt == "e4m3":
        words = by_word.astype(ml_dtypes.float8_e4m3fn).view(np.uint8)
    else:
        c = by_word.astype(ml_dtypes.float4_e2m1fn).view(np.uint8) & 0xF
        words = c[..., 0::2] | (c[..., 1::2] << 4)
    return np.ascontiguousarray(words), np.ascontiguousarray(byte.astype(np.uint8).reshape(k // 512, 16, n))


def unpack_weight(words, scales, fmt):
    g, p, n, _ = words.shape
    if fmt == "e4m3":
        vals = np.ascontiguousarray(words).view(ml_dtypes.float8_e4m3fn).astype(np.float64)
    else:
        nib = np.empty((g, p, n, 4), np.uint8)
        nib[..., 0::2] = words & 0xF
        nib[..., 1::2] = words >> 4
        vals = E2M1[nib]
    vals = vals * np.repeat(np.exp2(scales.astype(np.float64) - 127.0), 8, axis=1)[..., None]
    return vals.transpose(0, 1, 3, 2).reshape(g * 512, n)
def pack4(w):
    words, scales = pack_weight(w, "e2m1")
    return words.reshape(words.shape[0], 128, -1), scales


def unpack4(words, scales):
    return unpack_weight(words.reshape(words.shape[0], 128, -1, 2), scales, "e2m1")


N, K, IN, HID, OUT = 128, 32, 512, 512, 512
NEG_SLOPE = 0.01


def leaky_relu(v):
    return np.where(v >= 0, v, NEG_SLOPE * v)


def safediv(a, b):
    return a / np.where(b == 0, np.ones_like(b), b)


def draw0():
    s = mx_kscale(IN)
    u = mx_kscale(IN + HID)
    un, t = u[:IN], u[IN:]
    g = np.concatenate([np.full(IN, 1.0), np.full(HID, 3.0)])
    centre = np.random.standard_normal((N, 1, IN))
    h_node = bf(np.random.standard_normal((N, IN)) * un)
    h_ngbrs = bf((0.7 * centre + 0.7 * np.random.standard_normal((N, K, IN))) * s)
    alpha = bf(np.random.uniform(0.0, 1.0, (N, K, 1)))
    Wq = np.random.standard_normal((HID, IN)) / np.sqrt(IN) * t[:, None] / s[None, :]
    Wq_words, Wq_scales = pack4(Wq.T)
    bq = bf((-0.5 + 0.3 * np.random.standard_normal(HID)) * t)
    Ww = np.random.standard_normal((OUT, IN + HID)) * g[None, :] / np.sqrt(IN + HID) / u[None, :]
    Ww_words, Ww_scales = pack4(Ww.T)
    bw = bf(-0.8 + 0.3 * np.random.standard_normal(OUT))
    return {"h_node": h_node,
            "h_ngbrs": h_ngbrs,
            "alpha": alpha,
            "Wq_words": Wq_words,
            "Wq_scales": Wq_scales,
            "bq": bq,
            "Ww_words": Ww_words,
            "Ww_scales": Ww_scales,
            "bw": bw}


def core(h_node, h_ngbrs, alpha, Wq_words, Wq_scales, bq, Ww_words, Ww_scales, bw):
    a = f64(alpha)
    h1 = leaky_relu((mxq(f64(h_ngbrs), 2, "e4m3") @ unpack4(Wq_words, Wq_scales)) + f64(bq))
    h_agg = safediv((a * h1).sum(axis=1), a.sum(axis=1))
    h_concat = np.concatenate([f64(h_node), h_agg], axis=-1)
    h2 = leaky_relu((mxq(h_concat, 1, "e4m3") @ unpack4(Ww_words, Ww_scales)) + f64(bw))
    nrm = np.sqrt((h2 ** 2).sum(axis=-1, keepdims=True))
    return safediv(h2, nrm)


def e4m3fn_bytes(y):
    return np.clip(np.asarray(y, np.float64), -448.0, 448.0).astype(np.float32).astype(ml_dtypes.float8_e4m3fn).view(np.uint8)


def e4m3fn_values(b):
    return np.asarray(b, np.uint8).view(ml_dtypes.float8_e4m3fn).astype(np.float64)


def setup_inputs():
    d = draw0()
    x0 = np.asarray(d['h_ngbrs']).astype(np.float64)
    s = (np.max(np.abs(x0), axis=(0, 1), keepdims=True) / 448.0).astype(np.float32)
    out = {}
    for k, v in d.items():
        if k == 'h_ngbrs':
            out['h_ngbrs_bytes'] = e4m3fn_bytes(x0 / s.astype(np.float64))
            out['h_ngbrs_scale'] = s
        else:
            out[k] = v
    return out


def reference(h_node, h_ngbrs_bytes, h_ngbrs_scale, alpha, Wq_words, Wq_scales, bq, Ww_words, Ww_scales, bw):
    return core(h_node, e4m3fn_values(h_ngbrs_bytes) * h_ngbrs_scale.astype(np.float64), alpha, Wq_words, Wq_scales, bq, Ww_words, Ww_scales, bw)

@@ -1,0 +1,326 @@
+from contextlib import ExitStack
+
+import concourse.mybir as mybir
+from concourse.masks import make_identity
+
+F32 = mybir.dt.float32
+BF16 = mybir.dt.bfloat16
+I32 = mybir.dt.int32
+U32 = mybir.dt.uint32
+U8 = mybir.dt.uint8
+FP8 = mybir.dt.float8_e4m3fn
+FP8X4 = mybir.dt.float8_e4m3fn_x4
+FP4X4 = mybir.dt.float4_e2m1fn_x4
+ALU = mybir.AluOpType
+ACT = mybir.ActivationFunctionType
+AX = mybir.AxisListType
+
+P = 128
+K = 512
+NBR = 32
+PAIRS = NBR // 2
+SLOPE = 0.01
+FLOPS = 2 * 128 * 32 * 512 * 512 + 2 * 128 * 1024 * 512
+
+CHUNKS = (2, 2, 4, 8, 8, 8)
+
+
+def tile_pinsageconv_w4_kernel(
+    tc, h_node, h_ngbrs_bytes, h_ngbrs_scale, alpha, Wq_words, Wq_scales, bq, Ww_words, Ww_scales, bw, out
+):
+    nc = tc.nc
+    with ExitStack() as ctx:
+        keep = ctx.enter_context(tc.tile_pool(name="keep", bufs=1))
+        work = ctx.enter_context(tc.tile_pool(name="work", bufs=3))
+        pp = ctx.enter_context(tc.psum_pool(name="pp", bufs=5))
+        px = ctx.enter_context(tc.psum_pool(name="px", bufs=2))
+        pa = ctx.enter_context(tc.psum_pool(name="pa", bufs=1))
+        ctx.enter_context(tc.manual_schedule())
+
+        sc_col = keep.tile([P, 4], F32, name="sc_col")
+        bq_col = keep.tile([P, 4], BF16, name="bq_col")
+        bw_col = keep.tile([P, 4], BF16, name="bw_col")
+        al_bf = keep.tile([P, NBR], BF16, name="al_bf")
+        hn = keep.tile([P, K], BF16, name="hn")
+        wq = keep.tile([P, 1024], U8, name="wq", align_bytes=64)
+        wqs = keep.tile([P, 512], U8, name="wqs", align_bytes=64)
+        ww = keep.tile([P, 2, 1024], U8, name="ww", align_bytes=64)
+        wws = keep.tile([P, 2, 512], U8, name="wws", align_bytes=64)
+        ident = keep.tile([P, P], F32, name="ident")
+
+        make_identity(nc, ident[:])
+        nc.gpsimd.memset(wqs[:].bitcast(I32), 0)
+        nc.gpsimd.memset(wws[:].rearrange("p g n -> p (g n)").bitcast(I32), 0)
+
+        nc.sync.dma_start(out=sc_col[:], in_=h_ngbrs_scale.rearrange("a b (p c) -> p (a b c)", c=4))
+        nc.scalar.dma_start(out=al_bf[:], in_=alpha.rearrange("n k o -> n (k o)"))
+        nc.scalar.dma_start(out=bq_col[:], in_=bq.rearrange("(p t) -> p t", t=4))
+        nc.scalar.dma_start(out=bw_col[:], in_=bw.rearrange("(p t) -> p t", t=4))
+        nc.scalar.dma_start(out=hn[:], in_=h_node)
+
+        raw = []
+        k0 = 0
+        for i, n in enumerate(CHUNKS):
+            chunk = keep.tile([P, n * K], U8, name="raw%d" % i, align_bytes=64)
+            nc.sync.dma_start(out=chunk[:], in_=h_ngbrs_bytes[:, k0 : k0 + n, :].rearrange("n k f -> n (k f)"))
+            raw.extend([(chunk, j) for j in range(n)])
+            k0 += n
+            if i == 0:
+                nc.sync.dma_start(out=wq[:].bitcast(I32), in_=Wq_words[0].bitcast(I32))
+                for q in range(4):
+                    nc.sync.dma_start(
+                        out=wqs[32 * q : 32 * q + 4, :].bitcast(I32), in_=Wq_scales[0, 4 * q : 4 * q + 4, :].bitcast(I32)
+                    )
+        nc.sync.dma_start(out=ww[:].bitcast(I32), in_=Ww_words.rearrange("g p n -> p g n").bitcast(I32))
+        for q in range(4):
+            nc.sync.dma_start(
+                out=wws[32 * q : 32 * q + 4, :, :].bitcast(I32),
+                in_=Ww_scales[:, 4 * q : 4 * q + 4, :].rearrange("g q n -> q g n").bitcast(I32),
+            )
+
+        dummy = keep.tile([P, 1], F32, name="dummy")
+        nc.vector.memset(dummy[:], 1.0)
+        nc.scalar.activation(dummy[:], dummy[:], ACT.Sqrt)
+
+        al = keep.tile([P, NBR], F32, name="al")
+        asum = keep.tile([P, 1], F32, name="asum")
+        aden = keep.tile([P, 1], F32, name="aden")
+        arec = keep.tile([P, 1], F32, name="arec")
+        asig = keep.tile([P, 1], F32, name="asig")
+        c1 = keep.tile([P, NBR], F32, name="c1")
+        c2 = keep.tile([P, NBR], F32, name="c2")
+        bq32 = keep.tile([P, 4], F32, name="bq32")
+        bw32 = keep.tile([P, 4], F32, name="bw32")
+        nc.vector.tensor_copy(al[:], al_bf[:])
+        nc.vector.tensor_copy(bq32[:], bq_col[:])
+        nc.vector.reduce_sum(asum[:], al[:], axis=AX.X)
+        nc.vector.tensor_copy(bw32[:], bw_col[:])
+        nc.vector.scalar_tensor_tensor(aden[:], asum[:], 0.0, asum[:], op0=ALU.is_equal, op1=ALU.add)
+        nc.vector.reciprocal(arec[:], aden[:])
+        nc.vector.tensor_tensor(asig[:], asum[:], arec[:], op=ALU.mult)
+        nc.vector.tensor_scalar(c1[:], al[:], arec[:], SLOPE, op0=ALU.mult, op1=ALU.mult)
+        nc.vector.tensor_scalar(c2[:], al[:], arec[:], 1.0 - SLOPE, op0=ALU.mult, op1=ALU.mult)
+
+        def spread(col, name):
+            ps = pp.tile([P, 512], F32, name=name, tag="p")
+            for c in range(4):
+                nc.tensor.transpose(ps[:, 128 * c : 128 * (c + 1)], col[:, c : c + 1].to_broadcast([P, P]), ident[:])
+            return ps
+
+        sc2 = keep.tile([P, 2, K], F32, name="sc2")
+        sps = spread(sc_col, "sps")
+        inter = sps[:].rearrange("p (c i) -> p i c", c=4)
+        nc.vector.tensor_copy(sc2[:, 0, :].rearrange("p (i c) -> p i c", c=4), inter)
+        nc.scalar.copy(sc2[:, 1, :].rearrange("p (i c) -> p i c", c=4), inter)
+        sc_flat = sc2[:].rearrange("p a k -> p (a k)")
+
+        nb = keep.tile([P, 512], F32, name="nb")
+        bsig = keep.tile([P, 512], F32, name="bsig")
+        bwt = keep.tile([P, 512], F32, name="bwt")
+        bps = spread(bq32, "bps")
+        nc.scalar.activation(nb[:], bps[:], ACT.Copy, scale=-1.0)
+        nc.scalar.activation(bsig[:], bps[:], ACT.Copy, scale=asig[:])
+
+        xb = {}
+        xt = {}
+        grp = {}
+        codes = {}
+        scl = {}
+        pt = {}
+        zt = {}
+        lt = {}
+        st = {}
+
+        def prod(j, whole=True):
+            t = work.tile([P, 1024], BF16, name="xb", tag="xb", align_bytes=64)
+            xb[j] = t
+            chunk, i = raw[2 * j]
+            if whole:
+                nc.vector.tensor_tensor(
+                    t[:], chunk[:, i * K : (i + 2) * K].bitcast(FP8), sc_flat, op=ALU.mult
+                )
+            else:
+                for x in range(2):
+                    nc.vector.tensor_tensor(
+                        t[:, x * K : (x + 1) * K],
+                        chunk[:, (i + x) * K : (i + x + 1) * K].bitcast(FP8),
+                        sc2[:, 0, :],
+                        op=ALU.mult,
+                    )
+
+        def flip(j):
+            ps = px.tile([P, 512], F32, name="xt", tag="xt")
+            xt[j] = ps
+            words = xb[j][:].bitcast(F32)
+            for x in range(2):
+                for u in range(2):
+                    o = 128 * (2 * x + u)
+                    nc.tensor.transpose(ps[:, o : o + 128], words[:, 256 * x + u : 256 * (x + 1) : 2], ident[:])
+
+        def gather(j):
+            g = work.tile([P, 1024], BF16, name="grp", tag="grp", align_bytes=64)
+            grp[j] = g
+            nc.scalar.copy(
+                g[:].bitcast(F32).rearrange("p (x r u) -> p x r u", x=2, u=2),
+                xt[j][:].rearrange("p (x u r) -> p x r u", x=2, u=2),
+            )
+
+        def quant(j):
+            c = work.tile([P, 256], U32, name="codes", tag="codes", align_bytes=64)
+            s = work.tile([P, 256], U8, name="scl", tag="scl", align_bytes=64)
+            codes[j] = c
+            scl[j] = s
+            nc.vector.quantize_mx(out=c[:].bitcast(FP8X4), scales=s[:], in_=grp[j][:])
+
+        def mult(j):
+            for x in (1, 0):
+                ps = pp.tile([P, 512], F32, name="pt", tag="p")
+                pt[2 * j + x] = ps
+                cols = slice(128 * x, 128 * (x + 1))
+                nc.tensor.matmul_mx(
+                    out=ps[:],
+                    lhsT=codes[j][:, cols].bitcast(FP8X4),
+                    lhsT_scale=scl[j][:, cols],
+                    rhs=wq[:].bitcast(FP4X4),
+                    rhs_scale=wqs[:],
+                    start=True,
+                    stop=True,
+                )
+
+        def channels(ps):
+            return ps[:].rearrange("n (p t) -> n t p", t=4)
+
+        def planes(tile):
+            return tile[:].rearrange("n (t p) -> n t p", t=4)
+
+        def clip(k):
+            z = work.tile([P, 512], F32, name="z", tag="z%d" % (k % 2))
+            zt[k] = z
+            nc.vector.tensor_tensor(planes(z), channels(pt[k]), planes(nb), op=ALU.max)
+
+        def linear(k):
+            t = work.tile([P, 512], F32, name="l", tag="l%d" % (k % 2))
+            lt[k] = t
+            nc.scalar.activation(planes(t), channels(pt[k]), ACT.Copy, scale=c1[:, k : k + 1])
+
+        def weigh(k, on_vector):
+            t = work.tile([P, 512], F32, name="s", tag="s%d" % (k % 2))
+            st[k] = t
+            if on_vector:
+                nc.vector.tensor_scalar(t[:], zt[k][:], c2[:, k : k + 1], None, op0=ALU.mult)
+            else:
+                nc.scalar.activation(t[:], zt[k][:], ACT.Copy, scale=c2[:, k : k + 1])
+
+        acc = pa.tile([P, 512], F32, name="acc")
+
+        def add(tile, first=False, last=False):
+            for t in range(4):
+                nc.tensor.matmul(
+                    acc[:, 128 * t : 128 * (t + 1)],
+                    lhsT=tile[:, 128 * t : 128 * (t + 1)],
+                    rhs=ident[:],
+                    start=first and t == 0,
+                    stop=last and t == 3,
+                    is_transpose=True,
+                )
+
+        def reduce(j, last=False):
+            add(lt[2 * j])
+            add(lt[2 * j + 1])
+            add(st[2 * j + 1])
+            add(st[2 * j], last=last)
+
+        prod(0, whole=False)
+        flip(0)
+        gather(0)
+        prod(1)
+        quant(0)
+        flip(1)
+        prod(2)
+        mult(0)
+
+        hps = pp.tile([P, 512], F32, name="hps", tag="p")
+        hwords = hn[:].bitcast(F32)
+        for u in range(2):
+            nc.tensor.transpose(hps[:, 128 * u : 128 * (u + 1)], hwords[:, u:256:2], ident[:])
+        bwps = spread(bw32, "bwps")
+        gather(1)
+        hgrp = keep.tile([P, 512], BF16, name="hgrp", align_bytes=64)
+        nc.scalar.copy(
+            hgrp[:].bitcast(F32).rearrange("p (r u) -> p r u", u=2), hps[:, 0:256].rearrange("p (u r) -> p r u", u=2)
+        )
+        nc.scalar.copy(
+            bwt[:].rearrange("p (i c) -> p i c", c=4), bwps[:].rearrange("p (c i) -> p i c", c=4)
+        )
+        hcodes = keep.tile([P, 128], U32, name="hcodes", align_bytes=64)
+        hscl = keep.tile([P, 128], U8, name="hscl", align_bytes=64)
+        nc.vector.quantize_mx(out=hcodes[:].bitcast(FP8X4), scales=hscl[:], in_=hgrp[:])
+        add(bsig, first=True)
+
+        for r in range(PAIRS):
+            last = r == PAIRS - 1
+            on_vector = last or r % 3 == 1
+            if r + 2 < PAIRS:
+                flip(r + 2)
+            if r > 0:
+                reduce(r - 1)
+            clip(2 * r + 1)
+            clip(2 * r)
+            linear(2 * r)
+            linear(2 * r + 1)
+            weigh(2 * r + 1, last)
+            if r + 1 < PAIRS:
+                quant(r + 1)
+                mult(r + 1)
+            weigh(2 * r, on_vector)
+            if r + 3 < PAIRS:
+                prod(r + 3)
+            if r + 2 < PAIRS:
+                gather(r + 2)
+        reduce(PAIRS - 1, last=True)
+
+        p2 = pp.tile([P, 512], F32, name="p2", tag="p")
+
+        def mult2(g, c, s):
+            nc.tensor.matmul_mx(
+                out=p2[:],
+                lhsT=c[:].bitcast(FP8X4),
+                lhsT_scale=s[:],
+                rhs=ww[:, g, :].bitcast(FP4X4),
+                rhs_scale=wws[:, g, :],
+                start=g == 0,
+                stop=g == 1,
+            )
+
+        mult2(0, hcodes, hscl)
+        agrp = keep.tile([P, 512], BF16, name="agrp", align_bytes=64)
+        nc.scalar.copy(
+            agrp[:].rearrange("p (n t) -> p n t", t=4), acc[:].rearrange("p (t n) -> p n t", t=4)
+        )
+        acodes = keep.tile([P, 128], U32, name="acodes", align_bytes=64)
+        ascl = keep.tile([P, 128], U8, name="ascl", align_bytes=64)
+        nc.vector.quantize_mx(out=acodes[:].bitcast(FP8X4), scales=ascl[:], in_=agrp[:])
+        mult2(1, acodes, ascl)
+
+        t2 = keep.tile([P, 512], F32, name="t2")
+        y2 = keep.tile([P, 512], F32, name="y2")
+        sq = keep.tile([P, 512], F32, name="sq")
+        res = [keep.tile([P, 256], F32, name="res%d" % i) for i in range(2)]
+        ss = [keep.tile([P, 1], F32, name="ss%d" % i) for i in range(2)]
+        nrm = keep.tile([P, 1], F32, name="nrm")
+        nden = keep.tile([P, 1], F32, name="nden")
+        nrec = keep.tile([P, 1], F32, name="nrec")
+        halves = (slice(0, 256), slice(256, 512))
+        for h in halves:
+            nc.vector.tensor_tensor(t2[:, h], p2[:, h], bwt[:, h], op=ALU.add)
+        for h in halves:
+            nc.vector.scalar_tensor_tensor(y2[:, h], t2[:, h], SLOPE, t2[:, h], op0=ALU.mult, op1=ALU.max)
+        for i, h in enumerate(halves):
+            nc.scalar.activation(sq[:, h], y2[:, h], ACT.Square, accum_out=ss[i][:])
+        nc.scalar.activation(nrm[:], ss[0][:], ACT.Sqrt, bias=ss[1][:])
+        nc.vector.scalar_tensor_tensor(nden[:], nrm[:], 0.0, nrm[:], op0=ALU.is_equal, op1=ALU.add)
+        nc.vector.reciprocal(nrec[:], nden[:])
+        nc.vector.tensor_scalar(res[0][:], y2[:, halves[0]], nrec[:], None, op0=ALU.mult)
+        nc.scalar.activation(res[1][:], y2[:, halves[1]], ACT.Copy, scale=nrec[:])
+        nc.sync.dma_start(out=out[:, halves[0]], in_=res[0][:])
+        nc.scalar.dma_start(out=out[:, halves[1]], in_=res[1][:])

@@ -13,13 +13,13 @@ FP8X4 = mybir.dt.float8_e4m3fn_x4
 FP4X4 = mybir.dt.float4_e2m1fn_x4
 ALU = mybir.AluOpType
 ACT = mybir.ActivationFunctionType
-AX = mybir.AxisListType
 
 P = 128
 K = 512
 NBR = 32
 PAIRS = NBR // 2
 SLOPE = 0.01
+TINY = 2.0 ** -60
 FLOPS = 2 * 128 * 32 * 512 * 512 + 2 * 128 * 1024 * 512
 
 CHUNKS = (2, 2, 4, 8, 8, 8)
@@ -31,8 +31,8 @@ def tile_pinsageconv_w4_kernel(
     nc = tc.nc
     with ExitStack() as ctx:
         keep = ctx.enter_context(tc.tile_pool(name="keep", bufs=1))
-        work = ctx.enter_context(tc.tile_pool(name="work", bufs=3))
-        pp = ctx.enter_context(tc.psum_pool(name="pp", bufs=5))
+        work = ctx.enter_context(tc.tile_pool(name="work", bufs=4))
+        pp = ctx.enter_context(tc.psum_pool(name="pp", bufs=4))
         px = ctx.enter_context(tc.psum_pool(name="px", bufs=2))
         pa = ctx.enter_context(tc.psum_pool(name="pa", bufs=1))
         ctx.enter_context(tc.manual_schedule())
@@ -52,11 +52,11 @@ def tile_pinsageconv_w4_kernel(
         nc.gpsimd.memset(wqs[:].bitcast(I32), 0)
         nc.gpsimd.memset(wws[:].rearrange("p g n -> p (g n)").bitcast(I32), 0)
 
-        nc.sync.dma_start(out=sc_col[:], in_=h_ngbrs_scale.rearrange("a b (p c) -> p (a b c)", c=4))
+        nc.scalar.dma_start(out=sc_col[:], in_=h_ngbrs_scale.rearrange("a b (p c) -> p (a b c)", c=4))
         nc.scalar.dma_start(out=al_bf[:], in_=alpha.rearrange("n k o -> n (k o)"))
         nc.scalar.dma_start(out=bq_col[:], in_=bq.rearrange("(p t) -> p t", t=4))
-        nc.scalar.dma_start(out=bw_col[:], in_=bw.rearrange("(p t) -> p t", t=4))
         nc.scalar.dma_start(out=hn[:], in_=h_node)
+        nc.scalar.dma_start(out=bw_col[:], in_=bw.rearrange("(p t) -> p t", t=4))
 
         raw = []
         k0 = 0
@@ -80,26 +80,26 @@ def tile_pinsageconv_w4_kernel(
 
         dummy = keep.tile([P, 1], F32, name="dummy")
         nc.vector.memset(dummy[:], 1.0)
-        nc.scalar.activation(dummy[:], dummy[:], ACT.Sqrt)
+        nc.scalar.activation(dummy[:], dummy[:], ACT.Abs_reciprocal_sqrt)
 
         al = keep.tile([P, NBR], F32, name="al")
         asum = keep.tile([P, 1], F32, name="asum")
         aden = keep.tile([P, 1], F32, name="aden")
         arec = keep.tile([P, 1], F32, name="arec")
-        asig = keep.tile([P, 1], F32, name="asig")
+        nsig = keep.tile([P, 1], F32, name="nsig")
         c1 = keep.tile([P, NBR], F32, name="c1")
         c2 = keep.tile([P, NBR], F32, name="c2")
         bq32 = keep.tile([P, 4], F32, name="bq32")
         bw32 = keep.tile([P, 4], F32, name="bw32")
-        nc.vector.tensor_copy(al[:], al_bf[:])
-        nc.vector.tensor_copy(bq32[:], bq_col[:])
-        nc.vector.reduce_sum(asum[:], al[:], axis=AX.X)
-        nc.vector.tensor_copy(bw32[:], bw_col[:])
-        nc.vector.scalar_tensor_tensor(aden[:], asum[:], 0.0, asum[:], op0=ALU.is_equal, op1=ALU.add)
-        nc.vector.reciprocal(arec[:], aden[:])
-        nc.vector.tensor_tensor(asig[:], asum[:], arec[:], op=ALU.mult)
-        nc.vector.tensor_scalar(c1[:], al[:], arec[:], SLOPE, op0=ALU.mult, op1=ALU.mult)
-        nc.vector.tensor_scalar(c2[:], al[:], arec[:], 1.0 - SLOPE, op0=ALU.mult, op1=ALU.mult)
+        nc.gpsimd.tensor_copy(bq32[:], bq_col[:])
+        nc.gpsimd.tensor_copy(bw32[:], bw_col[:])
+
+        def weights():
+            nc.vector.scalar_tensor_tensor(aden[:], asum[:], 0.0, asum[:], op0=ALU.is_equal, op1=ALU.add)
+            nc.vector.reciprocal(arec[:], aden[:])
+            nc.gpsimd.tensor_scalar(c1[:], al[:], arec[:], SLOPE, op0=ALU.mult, op1=ALU.mult)
+            nc.gpsimd.tensor_scalar(c2[:], al[:], arec[:], 1.0 - SLOPE, op0=ALU.mult, op1=ALU.mult)
+            nc.vector.scalar_tensor_tensor(nsig[:], asum[:], -1.0, arec[:], op0=ALU.mult, op1=ALU.mult)
 
         def spread(col, name):
             ps = pp.tile([P, 512], F32, name=name, tag="p")
@@ -110,16 +110,25 @@ def tile_pinsageconv_w4_kernel(
         sc2 = keep.tile([P, 2, K], F32, name="sc2")
         sps = spread(sc_col, "sps")
         inter = sps[:].rearrange("p (c i) -> p i c", c=4)
-        nc.vector.tensor_copy(sc2[:, 0, :].rearrange("p (i c) -> p i c", c=4), inter)
+        nc.scalar.copy(sc2[:, 0, :].rearrange("p (i c) -> p i c", c=4), inter)
+        nc.scalar.activation(al[:], al_bf[:], ACT.Copy, accum_out=asum[:])
         nc.scalar.copy(sc2[:, 1, :].rearrange("p (i c) -> p i c", c=4), inter)
         sc_flat = sc2[:].rearrange("p a k -> p (a k)")
 
         nb = keep.tile([P, 512], F32, name="nb")
         bsig = keep.tile([P, 512], F32, name="bsig")
         bwt = keep.tile([P, 512], F32, name="bwt")
+        hps = pp.tile([P, 512], F32, name="hps", tag="p")
+        hwords = hn[:].bitcast(F32)
+        for u in range(2):
+            nc.tensor.transpose(hps[:, 128 * u : 128 * (u + 1)], hwords[:, u:256:2], ident[:])
+        hgrp = keep.tile([P, 512], BF16, name="hgrp", align_bytes=64)
+        nc.scalar.copy(
+            hgrp[:].bitcast(F32).rearrange("p (r u) -> p r u", u=2), hps[:, 0:256].rearrange("p (u r) -> p r u", u=2)
+        )
+        hcodes = keep.tile([P, 128], U32, name="hcodes", align_bytes=64)
+        hscl = keep.tile([P, 128], U8, name="hscl", align_bytes=64)
         bps = spread(bq32, "bps")
-        nc.scalar.activation(nb[:], bps[:], ACT.Copy, scale=-1.0)
-        nc.scalar.activation(bsig[:], bps[:], ACT.Copy, scale=asig[:])
 
         xb = {}
         xt = {}
@@ -203,11 +212,13 @@ def tile_pinsageconv_w4_kernel(
             lt[k] = t
             nc.scalar.activation(planes(t), channels(pt[k]), ACT.Copy, scale=c1[:, k : k + 1])
 
-        def weigh(k, on_vector):
+        def weigh(k, engine):
             t = work.tile([P, 512], F32, name="s", tag="s%d" % (k % 2))
             st[k] = t
-            if on_vector:
+            if engine == "vector":
                 nc.vector.tensor_scalar(t[:], zt[k][:], c2[:, k : k + 1], None, op0=ALU.mult)
+            elif engine == "gpsimd":
+                nc.gpsimd.tensor_scalar(t[:], zt[k][:], c2[:, k : k + 1], 0.0, op0=ALU.mult, op1=ALU.add)
             else:
                 nc.scalar.activation(t[:], zt[k][:], ACT.Copy, scale=c2[:, k : k + 1])
 
@@ -225,61 +236,13 @@ def tile_pinsageconv_w4_kernel(
                 )
 
         def reduce(j, last=False):
-            add(lt[2 * j])
-            add(lt[2 * j + 1])
+            if j < PAIRS - 3 or last:
+                add(lt[2 * j + 1], first=j == 0)
+                add(lt[2 * j])
             add(st[2 * j + 1])
             add(st[2 * j], last=last)
 
-        prod(0, whole=False)
-        flip(0)
-        gather(0)
-        prod(1)
-        quant(0)
-        flip(1)
-        prod(2)
-        mult(0)
-
-        hps = pp.tile([P, 512], F32, name="hps", tag="p")
-        hwords = hn[:].bitcast(F32)
-        for u in range(2):
-            nc.tensor.transpose(hps[:, 128 * u : 128 * (u + 1)], hwords[:, u:256:2], ident[:])
-        bwps = spread(bw32, "bwps")
-        gather(1)
-        hgrp = keep.tile([P, 512], BF16, name="hgrp", align_bytes=64)
-        nc.scalar.copy(
-            hgrp[:].bitcast(F32).rearrange("p (r u) -> p r u", u=2), hps[:, 0:256].rearrange("p (u r) -> p r u", u=2)
-        )
-        nc.scalar.copy(
-            bwt[:].rearrange("p (i c) -> p i c", c=4), bwps[:].rearrange("p (c i) -> p i c", c=4)
-        )
-        hcodes = keep.tile([P, 128], U32, name="hcodes", align_bytes=64)
-        hscl = keep.tile([P, 128], U8, name="hscl", align_bytes=64)
-        nc.vector.quantize_mx(out=hcodes[:].bitcast(FP8X4), scales=hscl[:], in_=hgrp[:])
-        add(bsig, first=True)
-
-        for r in range(PAIRS):
-            last = r == PAIRS - 1
-            on_vector = last or r % 3 == 1
-            if r + 2 < PAIRS:
-                flip(r + 2)
-            if r > 0:
-                reduce(r - 1)
-            clip(2 * r + 1)
-            clip(2 * r)
-            linear(2 * r)
-            linear(2 * r + 1)
-            weigh(2 * r + 1, last)
-            if r + 1 < PAIRS:
-                quant(r + 1)
-                mult(r + 1)
-            weigh(2 * r, on_vector)
-            if r + 3 < PAIRS:
-                prod(r + 3)
-            if r + 2 < PAIRS:
-                gather(r + 2)
-        reduce(PAIRS - 1, last=True)
-
-        p2 = pp.tile([P, 512], F32, name="p2", tag="p")
+        p2 = pp.tile([P, 512], F32, name="p2", tag="p2", bufs=1)
 
         def mult2(g, c, s):
             nc.tensor.matmul_mx(
@@ -292,7 +255,79 @@ def tile_pinsageconv_w4_kernel(
                 stop=g == 1,
             )
 
-        mult2(0, hcodes, hscl)
+        def bias():
+            nc.scalar.activation(nb[:], bps[:], ACT.Copy, scale=-1.0)
+
+        def extras(r):
+            if r == 1:
+                nc.scalar.activation(bsig[:], nb[:], ACT.Copy, scale=nsig[:])
+            if r == 2:
+                nc.vector.quantize_mx(out=hcodes[:].bitcast(FP8X4), scales=hscl[:], in_=hgrp[:])
+            if r == 3:
+                nc.scalar.copy(
+                    bwt[:].rearrange("p (i c) -> p i c", c=4), bwps[:].rearrange("p (c i) -> p i c", c=4)
+                )
+
+        def join(k):
+            t = work.tile([P, 512], F32, name="y", tag="y%d" % (k % 2))
+            nc.vector.scalar_tensor_tensor(
+                planes(t), channels(pt[k]), SLOPE / (1.0 - SLOPE), planes(zt[k]), op0=ALU.mult, op1=ALU.add
+            )
+            zt[k] = t
+
+
+        prod(0, whole=False)
+        flip(0)
+        gather(0)
+        bias()
+        prod(1)
+        weights()
+        quant(0)
+        flip(1)
+        prod(2)
+        mult(0)
+        gather(1)
+        quant(1)
+        prod(3)
+        flip(2)
+        gather(2)
+
+        for r in range(PAIRS):
+            tail = PAIRS - 3 <= r < PAIRS - 1
+            if r + 1 < PAIRS:
+                mult(r + 1)
+            if r == PAIRS - 2:
+                mult2(0, hcodes, hscl)
+            if r > 0:
+                reduce(r - 1)
+            if r == 1:
+                bwps = spread(bw32, "bwps")
+            if r == 3:
+                add(bsig)
+            if r + 3 < PAIRS:
+                flip(r + 3)
+            clip(2 * r + 1)
+            clip(2 * r)
+            if tail:
+                join(2 * r + 1)
+                join(2 * r)
+                weigh(2 * r + 1, "scalar")
+                weigh(2 * r, "scalar")
+            else:
+                linear(2 * r + 1)
+                linear(2 * r)
+                last = r == PAIRS - 1
+                weigh(2 * r + 1, "vector" if last else "gpsimd")
+                weigh(2 * r, "vector" if last else "scalar")
+            extras(r)
+            if r + 2 < PAIRS:
+                quant(r + 2)
+            if r + 4 < PAIRS:
+                prod(r + 4)
+            if r + 3 < PAIRS:
+                gather(r + 3)
+        reduce(PAIRS - 1, last=True)
+
         agrp = keep.tile([P, 512], BF16, name="agrp", align_bytes=64)
         nc.scalar.copy(
             agrp[:].rearrange("p (n t) -> p n t", t=4), acc[:].rearrange("p (t n) -> p n t", t=4)
@@ -303,23 +338,20 @@ def tile_pinsageconv_w4_kernel(
         mult2(1, acodes, ascl)
 
         t2 = keep.tile([P, 512], F32, name="t2")
-        y2 = keep.tile([P, 512], F32, name="y2")
-        sq = keep.tile([P, 512], F32, name="sq")
+        y2 = keep.tile([P, 512 + 1], F32, name="y2")
+        sq = keep.tile([P, 512 + 1], F32, name="sq")
         res = [keep.tile([P, 256], F32, name="res%d" % i) for i in range(2)]
         ss = [keep.tile([P, 1], F32, name="ss%d" % i) for i in range(2)]
-        nrm = keep.tile([P, 1], F32, name="nrm")
-        nden = keep.tile([P, 1], F32, name="nden")
         nrec = keep.tile([P, 1], F32, name="nrec")
+        nc.gpsimd.memset(y2[:, 512:], TINY)
         halves = (slice(0, 256), slice(256, 512))
         for h in halves:
             nc.vector.tensor_tensor(t2[:, h], p2[:, h], bwt[:, h], op=ALU.add)
         for h in halves:
             nc.vector.scalar_tensor_tensor(y2[:, h], t2[:, h], SLOPE, t2[:, h], op0=ALU.mult, op1=ALU.max)
-        for i, h in enumerate(halves):
+        for i, h in enumerate((slice(0, 256), slice(256, 513))):
             nc.scalar.activation(sq[:, h], y2[:, h], ACT.Square, accum_out=ss[i][:])
-        nc.scalar.activation(nrm[:], ss[0][:], ACT.Sqrt, bias=ss[1][:])
-        nc.vector.scalar_tensor_tensor(nden[:], nrm[:], 0.0, nrm[:], op0=ALU.is_equal, op1=ALU.add)
-        nc.vector.reciprocal(nrec[:], nden[:])
+        nc.scalar.activation(nrec[:], ss[0][:], ACT.Abs_reciprocal_sqrt, bias=ss[1][:])
         nc.vector.tensor_scalar(res[0][:], y2[:, halves[0]], nrec[:], None, op0=ALU.mult)
         nc.scalar.activation(res[1][:], y2[:, halves[1]], ACT.Copy, scale=nrec[:])
         nc.sync.dma_start(out=out[:, halves[0]], in_=res[0][:])

@@ -236,7 +236,7 @@ def tile_pinsageconv_w4_kernel(
                 )
 
         def reduce(j, last=False):
-            if j < PAIRS - 3 or last:
+            if j < PAIRS - 2 or last:
                 add(lt[2 * j + 1], first=j == 0)
                 add(lt[2 * j])
             add(st[2 * j + 1])
@@ -293,7 +293,7 @@ def tile_pinsageconv_w4_kernel(
         gather(2)
 
         for r in range(PAIRS):
-            tail = PAIRS - 3 <= r < PAIRS - 1
+            tail = PAIRS - 2 <= r < PAIRS - 1
             if r + 1 < PAIRS:
                 mult(r + 1)
             if r == PAIRS - 2:
@@ -317,7 +317,7 @@ def tile_pinsageconv_w4_kernel(
                 linear(2 * r + 1)
                 linear(2 * r)
                 last = r == PAIRS - 1
-                weigh(2 * r + 1, "vector" if last else "gpsimd")
+                weigh(2 * r + 1, "vector" if last else "vector" if r % 2 == 1 else "scalar")
                 weigh(2 * r, "vector" if last else "scalar")
             extras(r)
             if r + 2 < PAIRS:

@@ -49,6 +49,8 @@ def tile_pinsageconv_w4_kernel(
         ident = keep.tile([P, P], F32, name="ident")
 
         make_identity(nc, ident[:])
+        ident_bf = keep.tile([P, P], BF16, name="ident_bf")
+        nc.gpsimd.tensor_copy(ident_bf[:], ident[:])
         nc.gpsimd.memset(wqs[:].bitcast(I32), 0)
         nc.gpsimd.memset(wws[:].rearrange("p g n -> p (g n)").bitcast(I32), 0)
 
@@ -130,6 +132,9 @@ def tile_pinsageconv_w4_kernel(
         hscl = keep.tile([P, 128], U8, name="hscl", align_bytes=64)
         bps = spread(bq32, "bps")
 
+        def by_product(j):
+            return 3 <= j < 16
+
         xb = {}
         xt = {}
         grp = {}
@@ -140,16 +145,17 @@ def tile_pinsageconv_w4_kernel(
         lt = {}
         st = {}
 
-        def prod(j, whole=True):
-            t = work.tile([P, 1024], BF16, name="xb", tag="xb", align_bytes=64)
-            xb[j] = t
+        def prod(j, xs=None):
+            if j not in xb:
+                xb[j] = work.tile([P, 1024], BF16, name="xb", tag="xb", align_bytes=64)
+            t = xb[j]
             chunk, i = raw[2 * j]
-            if whole:
+            if xs is None:
                 nc.vector.tensor_tensor(
                     t[:], chunk[:, i * K : (i + 2) * K].bitcast(FP8), sc_flat, op=ALU.mult
                 )
             else:
-                for x in range(2):
+                for x in xs:
                     nc.vector.tensor_tensor(
                         t[:, x * K : (x + 1) * K],
                         chunk[:, (i + x) * K : (i + x + 1) * K].bitcast(FP8),
@@ -162,6 +168,16 @@ def tile_pinsageconv_w4_kernel(
             xt[j] = ps
             words = xb[j][:].bitcast(F32)
             for x in range(2):
+                if x == 0 and by_product(j):
+                    for t in range(4):
+                        nc.tensor.matmul(
+                            ps[:].bitcast(BF16)[:, 128 * t : 128 * (t + 1)],
+                            lhsT=xb[j][:, t:512:4],
+                            rhs=ident_bf[:],
+                            start=True,
+                            stop=True,
+                        )
+                    continue
                 for u in range(2):
                     o = 128 * (2 * x + u)
                     nc.tensor.transpose(ps[:, o : o + 128], words[:, 256 * x + u : 256 * (x + 1) : 2], ident[:])
@@ -169,6 +185,16 @@ def tile_pinsageconv_w4_kernel(
         def gather(j):
             g = work.tile([P, 1024], BF16, name="grp", tag="grp", align_bytes=64)
             grp[j] = g
+            if by_product(j):
+                nc.scalar.copy(
+                    g[:, 0:512].rearrange("p (r t) -> p r t", t=4),
+                    xt[j][:].bitcast(BF16)[:, 0:512].rearrange("p (t r) -> p r t", t=4),
+                )
+                nc.scalar.copy(
+                    g[:, 512:1024].bitcast(F32).rearrange("p (r u) -> p r u", u=2),
+                    xt[j][:, 256:512].rearrange("p (u r) -> p r u", u=2),
+                )
+                return
             nc.scalar.copy(
                 g[:].bitcast(F32).rearrange("p (x r u) -> p x r u", x=2, u=2),
                 xt[j][:].rearrange("p (x u r) -> p x r u", x=2, u=2),
@@ -235,12 +261,20 @@ def tile_pinsageconv_w4_kernel(
                     is_transpose=True,
                 )
 
-        def reduce(j, last=False):
-            if j < PAIRS - 2 or last:
-                add(lt[2 * j + 1], first=j == 0)
-                add(lt[2 * j])
-            add(st[2 * j + 1])
-            add(st[2 * j], last=last)
+        def one_piece(j):
+            return PAIRS - 3 <= j < PAIRS - 1
+
+        def reduce(j, half):
+            if half == 0:
+                if one_piece(j):
+                    add(st[2 * j + 1])
+                else:
+                    add(lt[2 * j + 1], first=j == 0)
+                    add(lt[2 * j])
+            else:
+                if not one_piece(j):
+                    add(st[2 * j + 1])
+                add(st[2 * j], last=j == PAIRS - 1)
 
         p2 = pp.tile([P, 512], F32, name="p2", tag="p2", bufs=1)
 
@@ -276,7 +310,7 @@ def tile_pinsageconv_w4_kernel(
             zt[k] = t
 
 
-        prod(0, whole=False)
+        prod(0, (0, 1))
         flip(0)
         gather(0)
         bias()
@@ -293,22 +327,23 @@ def tile_pinsageconv_w4_kernel(
         gather(2)
 
         for r in range(PAIRS):
-            tail = PAIRS - 2 <= r < PAIRS - 1
             if r + 1 < PAIRS:
                 mult(r + 1)
             if r == PAIRS - 2:
                 mult2(0, hcodes, hscl)
             if r > 0:
-                reduce(r - 1)
+                reduce(r - 1, 0)
+            if r + 3 < PAIRS and True:
+                flip(r + 3)
             if r == 1:
                 bwps = spread(bw32, "bwps")
             if r == 3:
                 add(bsig)
-            if r + 3 < PAIRS:
-                flip(r + 3)
+            if r > 0:
+                reduce(r - 1, 1)
             clip(2 * r + 1)
             clip(2 * r)
-            if tail:
+            if one_piece(r):
                 join(2 * r + 1)
                 join(2 * r)
                 weigh(2 * r + 1, "scalar")
@@ -317,7 +352,7 @@ def tile_pinsageconv_w4_kernel(
                 linear(2 * r + 1)
                 linear(2 * r)
                 last = r == PAIRS - 1
-                weigh(2 * r + 1, "vector" if last else "vector" if r % 2 == 1 else "scalar")
+                weigh(2 * r + 1, "vector" if last else "vector")
                 weigh(2 * r, "vector" if last else "scalar")
             extras(r)
             if r + 2 < PAIRS:
@@ -326,7 +361,8 @@ def tile_pinsageconv_w4_kernel(
                 prod(r + 4)
             if r + 3 < PAIRS:
                 gather(r + 3)
-        reduce(PAIRS - 1, last=True)
+        reduce(PAIRS - 1, 0)
+        reduce(PAIRS - 1, 1)
 
         agrp = keep.tile([P, 512], BF16, name="agrp", align_bytes=64)
         nc.scalar.copy(

@@ -15,14 +15,29 @@ ALU = mybir.AluOpType
 ACT = mybir.ActivationFunctionType
 
 P = 128
-K = 512
-NBR = 32
-PAIRS = NBR // 2
+FEATURES = 512
+PACK = 4
+NEIGHBOURS = 32
+PAIRS = NEIGHBOURS // 2
 SLOPE = 0.01
-TINY = 2.0 ** -60
-FLOPS = 2 * 128 * 32 * 512 * 512 + 2 * 128 * 1024 * 512
+TINY = 2.0**-60
 
-CHUNKS = (2, 2, 4, 8, 8, 8)
+LOADS = (2, 2, 4, 8, 8, 8)
+
+SCALE_AHEAD = 4
+TURN_AHEAD = 3
+QUANT_AHEAD = 2
+MULT_AHEAD = 1
+
+FLOPS = 2 * P * NEIGHBOURS * FEATURES * FEATURES + 2 * P * (2 * FEATURES) * FEATURES
+
+
+def turned_by_matmul(j):
+    return 2 < j < 15 and j % 3 != 0
+
+
+def joined(j):
+    return j == PAIRS - 2
 
 
 def tile_pinsageconv_w4_kernel(
@@ -32,363 +47,337 @@ def tile_pinsageconv_w4_kernel(
     with ExitStack() as ctx:
         keep = ctx.enter_context(tc.tile_pool(name="keep", bufs=1))
         work = ctx.enter_context(tc.tile_pool(name="work", bufs=4))
-        pp = ctx.enter_context(tc.psum_pool(name="pp", bufs=4))
-        px = ctx.enter_context(tc.psum_pool(name="px", bufs=2))
-        pa = ctx.enter_context(tc.psum_pool(name="pa", bufs=1))
+        products = ctx.enter_context(tc.psum_pool(name="products", bufs=4))
+        turned_pool = ctx.enter_context(tc.psum_pool(name="turned_pool", bufs=2))
+        single = ctx.enter_context(tc.psum_pool(name="single", bufs=1))
         ctx.enter_context(tc.manual_schedule())
 
-        sc_col = keep.tile([P, 4], F32, name="sc_col")
-        bq_col = keep.tile([P, 4], BF16, name="bq_col")
-        bw_col = keep.tile([P, 4], BF16, name="bw_col")
-        al_bf = keep.tile([P, NBR], BF16, name="al_bf")
-        hn = keep.tile([P, K], BF16, name="hn")
-        wq = keep.tile([P, 1024], U8, name="wq", align_bytes=64)
-        wqs = keep.tile([P, 512], U8, name="wqs", align_bytes=64)
-        ww = keep.tile([P, 2, 1024], U8, name="ww", align_bytes=64)
-        wws = keep.tile([P, 2, 512], U8, name="wws", align_bytes=64)
         ident = keep.tile([P, P], F32, name="ident")
-
-        make_identity(nc, ident[:])
         ident_bf = keep.tile([P, P], BF16, name="ident_bf")
+        make_identity(nc, ident[:])
         nc.gpsimd.tensor_copy(ident_bf[:], ident[:])
-        nc.gpsimd.memset(wqs[:].bitcast(I32), 0)
-        nc.gpsimd.memset(wws[:].rearrange("p g n -> p (g n)").bitcast(I32), 0)
 
-        nc.scalar.dma_start(out=sc_col[:], in_=h_ngbrs_scale.rearrange("a b (p c) -> p (a b c)", c=4))
-        nc.scalar.dma_start(out=al_bf[:], in_=alpha.rearrange("n k o -> n (k o)"))
-        nc.scalar.dma_start(out=bq_col[:], in_=bq.rearrange("(p t) -> p t", t=4))
-        nc.scalar.dma_start(out=hn[:], in_=h_node)
-        nc.scalar.dma_start(out=bw_col[:], in_=bw.rearrange("(p t) -> p t", t=4))
+        wq_scales = keep.tile([P, FEATURES], U8, name="wq_scales", align_bytes=64)
+        ww_scales = keep.tile([P, 2, FEATURES], U8, name="ww_scales", align_bytes=64)
+        nc.gpsimd.memset(wq_scales[:].bitcast(I32), 0)
+        nc.gpsimd.memset(ww_scales[:].rearrange("p g n -> p (g n)").bitcast(I32), 0)
 
-        raw = []
-        k0 = 0
-        for i, n in enumerate(CHUNKS):
-            chunk = keep.tile([P, n * K], U8, name="raw%d" % i, align_bytes=64)
-            nc.sync.dma_start(out=chunk[:], in_=h_ngbrs_bytes[:, k0 : k0 + n, :].rearrange("n k f -> n (k f)"))
-            raw.extend([(chunk, j) for j in range(n)])
-            k0 += n
+        x_scale = keep.tile([P, PACK], F32, name="x_scale")
+        alpha_bf = keep.tile([P, NEIGHBOURS], BF16, name="alpha_bf")
+        bq_bf = keep.tile([P, PACK], BF16, name="bq_bf")
+        node = keep.tile([P, FEATURES], BF16, name="node")
+        bw_bf = keep.tile([P, PACK], BF16, name="bw_bf")
+        nc.scalar.dma_start(out=x_scale[:], in_=h_ngbrs_scale.rearrange("a b (p t) -> p (a b t)", t=PACK))
+        nc.scalar.dma_start(out=alpha_bf[:], in_=alpha.rearrange("n k o -> n (k o)"))
+        nc.scalar.dma_start(out=bq_bf[:], in_=bq.rearrange("(p t) -> p t", t=PACK))
+        nc.scalar.dma_start(out=node[:], in_=h_node)
+        nc.scalar.dma_start(out=bw_bf[:], in_=bw.rearrange("(p t) -> p t", t=PACK))
+
+        wq_words = keep.tile([P, 2 * FEATURES], U8, name="wq_words", align_bytes=64)
+        ww_words = keep.tile([P, 2, 2 * FEATURES], U8, name="ww_words", align_bytes=64)
+        token_bytes = []
+        for i, count in enumerate(LOADS):
+            first_k = len(token_bytes)
+            loaded = keep.tile([P, count * FEATURES], U8, name="loaded%d" % i, align_bytes=64)
+            nc.sync.dma_start(
+                out=loaded[:], in_=h_ngbrs_bytes[:, first_k : first_k + count, :].rearrange("n k f -> n (k f)")
+            )
+            token_bytes.extend([(loaded, place) for place in range(count)])
             if i == 0:
-                nc.sync.dma_start(out=wq[:].bitcast(I32), in_=Wq_words[0].bitcast(I32))
+                nc.sync.dma_start(out=wq_words[:].bitcast(I32), in_=Wq_words[0].bitcast(I32))
                 for q in range(4):
                     nc.sync.dma_start(
-                        out=wqs[32 * q : 32 * q + 4, :].bitcast(I32), in_=Wq_scales[0, 4 * q : 4 * q + 4, :].bitcast(I32)
+                        out=wq_scales[32 * q : 32 * q + 4, :].bitcast(I32),
+                        in_=Wq_scales[0, 4 * q : 4 * q + 4, :].bitcast(I32),
                     )
-        nc.sync.dma_start(out=ww[:].bitcast(I32), in_=Ww_words.rearrange("g p n -> p g n").bitcast(I32))
+        nc.sync.dma_start(out=ww_words[:].bitcast(I32), in_=Ww_words.rearrange("g p n -> p g n").bitcast(I32))
         for q in range(4):
             nc.sync.dma_start(
-                out=wws[32 * q : 32 * q + 4, :, :].bitcast(I32),
+                out=ww_scales[32 * q : 32 * q + 4, :, :].bitcast(I32),
                 in_=Ww_scales[:, 4 * q : 4 * q + 4, :].rearrange("g q n -> q g n").bitcast(I32),
             )
 
-        dummy = keep.tile([P, 1], F32, name="dummy")
-        nc.vector.memset(dummy[:], 1.0)
-        nc.scalar.activation(dummy[:], dummy[:], ACT.Abs_reciprocal_sqrt)
+        table = keep.tile([P, 1], F32, name="table")
+        nc.vector.memset(table[:], 1.0)
+        nc.scalar.activation(table[:], table[:], ACT.Abs_reciprocal_sqrt)
 
-        al = keep.tile([P, NBR], F32, name="al")
-        asum = keep.tile([P, 1], F32, name="asum")
-        aden = keep.tile([P, 1], F32, name="aden")
-        arec = keep.tile([P, 1], F32, name="arec")
-        nsig = keep.tile([P, 1], F32, name="nsig")
-        c1 = keep.tile([P, NBR], F32, name="c1")
-        c2 = keep.tile([P, NBR], F32, name="c2")
-        bq32 = keep.tile([P, 4], F32, name="bq32")
-        bw32 = keep.tile([P, 4], F32, name="bw32")
-        nc.gpsimd.tensor_copy(bq32[:], bq_col[:])
-        nc.gpsimd.tensor_copy(bw32[:], bw_col[:])
-
-        def weights():
-            nc.vector.scalar_tensor_tensor(aden[:], asum[:], 0.0, asum[:], op0=ALU.is_equal, op1=ALU.add)
-            nc.vector.reciprocal(arec[:], aden[:])
-            nc.gpsimd.tensor_scalar(c1[:], al[:], arec[:], SLOPE, op0=ALU.mult, op1=ALU.mult)
-            nc.gpsimd.tensor_scalar(c2[:], al[:], arec[:], 1.0 - SLOPE, op0=ALU.mult, op1=ALU.mult)
-            nc.vector.scalar_tensor_tensor(nsig[:], asum[:], -1.0, arec[:], op0=ALU.mult, op1=ALU.mult)
-
-        def spread(col, name):
-            ps = pp.tile([P, 512], F32, name=name, tag="p")
-            for c in range(4):
-                nc.tensor.transpose(ps[:, 128 * c : 128 * (c + 1)], col[:, c : c + 1].to_broadcast([P, P]), ident[:])
-            return ps
-
-        sc2 = keep.tile([P, 2, K], F32, name="sc2")
-        sps = spread(sc_col, "sps")
-        inter = sps[:].rearrange("p (c i) -> p i c", c=4)
-        nc.scalar.copy(sc2[:, 0, :].rearrange("p (i c) -> p i c", c=4), inter)
-        nc.scalar.activation(al[:], al_bf[:], ACT.Copy, accum_out=asum[:])
-        nc.scalar.copy(sc2[:, 1, :].rearrange("p (i c) -> p i c", c=4), inter)
-        sc_flat = sc2[:].rearrange("p a k -> p (a k)")
-
-        nb = keep.tile([P, 512], F32, name="nb")
-        bsig = keep.tile([P, 512], F32, name="bsig")
-        bwt = keep.tile([P, 512], F32, name="bwt")
-        hps = pp.tile([P, 512], F32, name="hps", tag="p")
-        hwords = hn[:].bitcast(F32)
-        for u in range(2):
-            nc.tensor.transpose(hps[:, 128 * u : 128 * (u + 1)], hwords[:, u:256:2], ident[:])
-        hgrp = keep.tile([P, 512], BF16, name="hgrp", align_bytes=64)
-        nc.scalar.copy(
-            hgrp[:].bitcast(F32).rearrange("p (r u) -> p r u", u=2), hps[:, 0:256].rearrange("p (u r) -> p r u", u=2)
-        )
-        hcodes = keep.tile([P, 128], U32, name="hcodes", align_bytes=64)
-        hscl = keep.tile([P, 128], U8, name="hscl", align_bytes=64)
-        bps = spread(bq32, "bps")
-
-        def by_product(j):
-            return 3 <= j < 16
-
-        xb = {}
-        xt = {}
-        grp = {}
-        codes = {}
-        scl = {}
-        pt = {}
-        zt = {}
-        lt = {}
-        st = {}
-
-        def prod(j, xs=None):
-            if j not in xb:
-                xb[j] = work.tile([P, 1024], BF16, name="xb", tag="xb", align_bytes=64)
-            t = xb[j]
-            chunk, i = raw[2 * j]
-            if xs is None:
-                nc.vector.tensor_tensor(
-                    t[:], chunk[:, i * K : (i + 2) * K].bitcast(FP8), sc_flat, op=ALU.mult
+        def spread(column_tile, name):
+            bank = products.tile([P, FEATURES], F32, name=name, tag="product")
+            for t in range(PACK):
+                nc.tensor.transpose(
+                    bank[:, P * t : P * (t + 1)], column_tile[:, t : t + 1].to_broadcast([P, P]), ident[:]
                 )
-            else:
-                for x in xs:
-                    nc.vector.tensor_tensor(
-                        t[:, x * K : (x + 1) * K],
-                        chunk[:, (i + x) * K : (i + x + 1) * K].bitcast(FP8),
-                        sc2[:, 0, :],
-                        op=ALU.mult,
-                    )
+            return bank
 
-        def flip(j):
-            ps = px.tile([P, 512], F32, name="xt", tag="xt")
-            xt[j] = ps
-            words = xb[j][:].bitcast(F32)
+        def plain_order(bank):
+            return bank[:].rearrange("p (t i) -> p i t", t=PACK)
+
+        bq_f32 = keep.tile([P, PACK], F32, name="bq_f32")
+        bw_f32 = keep.tile([P, PACK], F32, name="bw_f32")
+        nc.gpsimd.tensor_copy(bq_f32[:], bq_bf[:])
+        nc.gpsimd.tensor_copy(bw_f32[:], bw_bf[:])
+
+        scale_row = keep.tile([P, 2, FEATURES], F32, name="scale_row")
+        alpha_f32 = keep.tile([P, NEIGHBOURS], F32, name="alpha_f32")
+        alpha_sum = keep.tile([P, 1], F32, name="alpha_sum")
+        scale_bank = spread(x_scale, "scale_bank")
+        nc.scalar.copy(scale_row[:, 0, :].rearrange("p (i t) -> p i t", t=PACK), plain_order(scale_bank))
+        nc.scalar.activation(alpha_f32[:], alpha_bf[:], ACT.Copy, accum_out=alpha_sum[:])
+        nc.scalar.copy(scale_row[:, 1, :].rearrange("p (i t) -> p i t", t=PACK), plain_order(scale_bank))
+
+        node_bank = products.tile([P, FEATURES], F32, name="node_bank", tag="product")
+        node_words = node[:].bitcast(F32)
+        for u in range(2):
+            nc.tensor.transpose(node_bank[:, P * u : P * (u + 1)], node_words[:, u : FEATURES // 2 : 2], ident[:])
+        node_grouped = keep.tile([P, FEATURES], BF16, name="node_grouped", align_bytes=64)
+        nc.scalar.copy(
+            node_grouped[:].bitcast(F32).rearrange("p (n u) -> p n u", u=2),
+            node_bank[:, : FEATURES // 2].rearrange("p (u n) -> p n u", u=2),
+        )
+        bq_bank = spread(bq_f32, "bq_bank")
+        bw_bank = spread(bw_f32, "bw_bank")
+
+        scaled, turned, grouped, codes, code_scales = {}, {}, {}, {}, {}
+        product, clipped, linear_piece, weighed_piece = {}, {}, {}, {}
+
+        def scale(j, separately=False):
+            scaled[j] = work.tile([P, 2 * FEATURES], BF16, name="scaled", tag="scaled", align_bytes=64)
+            loaded, place = token_bytes[2 * j]
+            for start, stop in ((0, 1), (1, 2)) if separately else ((0, 2),):
+                nc.vector.tensor_tensor(
+                    scaled[j][:, start * FEATURES : stop * FEATURES],
+                    loaded[:, (place + start) * FEATURES : (place + stop) * FEATURES].bitcast(FP8),
+                    scale_row[:, 0 : stop - start, :].rearrange("p x f -> p (x f)"),
+                    op=ALU.mult,
+                )
+
+        def turn(j):
+            turned[j] = turned_pool.tile([P, 2 * FEATURES // 2], F32, name="turned", tag="turned")
+            words = scaled[j][:].bitcast(F32)
+            half = FEATURES // 2
             for x in range(2):
-                if x == 0 and by_product(j):
-                    for t in range(4):
+                if x == 0 and turned_by_matmul(j):
+                    for t in range(PACK):
                         nc.tensor.matmul(
-                            ps[:].bitcast(BF16)[:, 128 * t : 128 * (t + 1)],
-                            lhsT=xb[j][:, t:512:4],
+                            turned[j][:].bitcast(BF16)[:, P * t : P * (t + 1)],
+                            lhsT=scaled[j][:, t:FEATURES:PACK],
                             rhs=ident_bf[:],
                             start=True,
                             stop=True,
                         )
-                    continue
-                for u in range(2):
-                    o = 128 * (2 * x + u)
-                    nc.tensor.transpose(ps[:, o : o + 128], words[:, 256 * x + u : 256 * (x + 1) : 2], ident[:])
+                else:
+                    for u in range(2):
+                        place = half * x + P * u
+                        nc.tensor.transpose(
+                            turned[j][:, place : place + P], words[:, half * x + u : half * (x + 1) : 2], ident[:]
+                        )
 
-        def gather(j):
-            g = work.tile([P, 1024], BF16, name="grp", tag="grp", align_bytes=64)
-            grp[j] = g
-            if by_product(j):
+        def interleave(j):
+            grouped[j] = work.tile([P, 2 * FEATURES], BF16, name="grouped", tag="grouped", align_bytes=64)
+            half = FEATURES // 2
+            if turned_by_matmul(j):
                 nc.scalar.copy(
-                    g[:, 0:512].rearrange("p (r t) -> p r t", t=4),
-                    xt[j][:].bitcast(BF16)[:, 0:512].rearrange("p (t r) -> p r t", t=4),
+                    grouped[j][:, :FEATURES].rearrange("p (n t) -> p n t", t=PACK),
+                    turned[j][:].bitcast(BF16)[:, :FEATURES].rearrange("p (t n) -> p n t", t=PACK),
                 )
                 nc.scalar.copy(
-                    g[:, 512:1024].bitcast(F32).rearrange("p (r u) -> p r u", u=2),
-                    xt[j][:, 256:512].rearrange("p (u r) -> p r u", u=2),
+                    grouped[j][:, FEATURES:].bitcast(F32).rearrange("p (n u) -> p n u", u=2),
+                    turned[j][:, half:].rearrange("p (u n) -> p n u", u=2),
                 )
-                return
-            nc.scalar.copy(
-                g[:].bitcast(F32).rearrange("p (x r u) -> p x r u", x=2, u=2),
-                xt[j][:].rearrange("p (x u r) -> p x r u", x=2, u=2),
-            )
+            else:
+                nc.scalar.copy(
+                    grouped[j][:].bitcast(F32).rearrange("p (x n u) -> p x n u", x=2, u=2),
+                    turned[j][:].rearrange("p (x u n) -> p x n u", x=2, u=2),
+                )
 
-        def quant(j):
-            c = work.tile([P, 256], U32, name="codes", tag="codes", align_bytes=64)
-            s = work.tile([P, 256], U8, name="scl", tag="scl", align_bytes=64)
-            codes[j] = c
-            scl[j] = s
-            nc.vector.quantize_mx(out=c[:].bitcast(FP8X4), scales=s[:], in_=grp[j][:])
+        def quantise(j):
+            codes[j] = work.tile([P, 2 * P], U32, name="codes", tag="codes", align_bytes=64)
+            code_scales[j] = work.tile([P, 2 * P], U8, name="code_scales", tag="code_scales", align_bytes=64)
+            nc.vector.quantize_mx(out=codes[j][:].bitcast(FP8X4), scales=code_scales[j][:], in_=grouped[j][:])
 
-        def mult(j):
+        def multiply(j):
             for x in (1, 0):
-                ps = pp.tile([P, 512], F32, name="pt", tag="p")
-                pt[2 * j + x] = ps
-                cols = slice(128 * x, 128 * (x + 1))
+                bank = products.tile([P, FEATURES], F32, name="product", tag="product")
+                product[2 * j + x] = bank
+                nodes = slice(P * x, P * (x + 1))
                 nc.tensor.matmul_mx(
-                    out=ps[:],
-                    lhsT=codes[j][:, cols].bitcast(FP8X4),
-                    lhsT_scale=scl[j][:, cols],
-                    rhs=wq[:].bitcast(FP4X4),
-                    rhs_scale=wqs[:],
+                    out=bank[:],
+                    lhsT=codes[j][:, nodes].bitcast(FP8X4),
+                    lhsT_scale=code_scales[j][:, nodes],
+                    rhs=wq_words[:].bitcast(FP4X4),
+                    rhs_scale=wq_scales[:],
                     start=True,
                     stop=True,
                 )
 
-        def channels(ps):
-            return ps[:].rearrange("n (p t) -> n t p", t=4)
+        def channels(bank):
+            return bank[:].rearrange("n (p t) -> n t p", t=PACK)
 
-        def planes(tile):
-            return tile[:].rearrange("n (t p) -> n t p", t=4)
+        def planes(piece):
+            return piece[:].rearrange("n (t p) -> n t p", t=PACK)
 
         def clip(k):
-            z = work.tile([P, 512], F32, name="z", tag="z%d" % (k % 2))
-            zt[k] = z
-            nc.vector.tensor_tensor(planes(z), channels(pt[k]), planes(nb), op=ALU.max)
+            clipped[k] = work.tile([P, FEATURES], F32, name="clipped", tag="clipped%d" % (k % 2))
+            nc.vector.tensor_tensor(planes(clipped[k]), channels(product[k]), planes(minus_bq), op=ALU.max)
 
         def linear(k):
-            t = work.tile([P, 512], F32, name="l", tag="l%d" % (k % 2))
-            lt[k] = t
-            nc.scalar.activation(planes(t), channels(pt[k]), ACT.Copy, scale=c1[:, k : k + 1])
+            linear_piece[k] = work.tile([P, FEATURES], F32, name="linear_piece", tag="linear%d" % (k % 2))
+            nc.scalar.activation(planes(linear_piece[k]), channels(product[k]), ACT.Copy, scale=a_slope[:, k : k + 1])
 
-        def weigh(k, engine):
-            t = work.tile([P, 512], F32, name="s", tag="s%d" % (k % 2))
-            st[k] = t
-            if engine == "vector":
-                nc.vector.tensor_scalar(t[:], zt[k][:], c2[:, k : k + 1], None, op0=ALU.mult)
-            elif engine == "gpsimd":
-                nc.gpsimd.tensor_scalar(t[:], zt[k][:], c2[:, k : k + 1], 0.0, op0=ALU.mult, op1=ALU.add)
+        def join(k):
+            both = work.tile([P, FEATURES], F32, name="both", tag="both%d" % (k % 2))
+            nc.vector.scalar_tensor_tensor(
+                planes(both), channels(product[k]), SLOPE / (1.0 - SLOPE), planes(clipped[k]), op0=ALU.mult, op1=ALU.add
+            )
+            clipped[k] = both
+
+        def weigh(k, by_vector=False):
+            weighed_piece[k] = work.tile([P, FEATURES], F32, name="weighed_piece", tag="weighed%d" % (k % 2))
+            factor = a_rest[:, k : k + 1]
+            if by_vector:
+                nc.vector.tensor_scalar(weighed_piece[k][:], clipped[k][:], factor, None, op0=ALU.mult)
             else:
-                nc.scalar.activation(t[:], zt[k][:], ACT.Copy, scale=c2[:, k : k + 1])
+                nc.scalar.activation(weighed_piece[k][:], clipped[k][:], ACT.Copy, scale=factor)
 
-        acc = pa.tile([P, 512], F32, name="acc")
+        mean = single.tile([P, FEATURES], F32, name="mean")
 
-        def add(tile, first=False, last=False):
-            for t in range(4):
+        def add(piece, first=False, last=False):
+            for t in range(PACK):
                 nc.tensor.matmul(
-                    acc[:, 128 * t : 128 * (t + 1)],
-                    lhsT=tile[:, 128 * t : 128 * (t + 1)],
+                    mean[:, P * t : P * (t + 1)],
+                    lhsT=piece[:, P * t : P * (t + 1)],
                     rhs=ident[:],
                     start=first and t == 0,
-                    stop=last and t == 3,
+                    stop=last and t == PACK - 1,
                     is_transpose=True,
                 )
 
-        def one_piece(j):
-            return PAIRS - 3 <= j < PAIRS - 1
-
-        def reduce(j, half):
-            if half == 0:
-                if one_piece(j):
-                    add(st[2 * j + 1])
-                else:
-                    add(lt[2 * j + 1], first=j == 0)
-                    add(lt[2 * j])
+        def add_first_half(j):
+            if joined(j):
+                add(weighed_piece[2 * j + 1])
             else:
-                if not one_piece(j):
-                    add(st[2 * j + 1])
-                add(st[2 * j], last=j == PAIRS - 1)
+                add(linear_piece[2 * j + 1], first=j == 0)
+                add(linear_piece[2 * j])
 
-        p2 = pp.tile([P, 512], F32, name="p2", tag="p2", bufs=1)
+        def add_second_half(j):
+            if not joined(j):
+                add(weighed_piece[2 * j + 1])
+            add(weighed_piece[2 * j], last=j == PAIRS - 1)
 
-        def mult2(g, c, s):
-            nc.tensor.matmul_mx(
-                out=p2[:],
-                lhsT=c[:].bitcast(FP8X4),
-                lhsT_scale=s[:],
-                rhs=ww[:, g, :].bitcast(FP4X4),
-                rhs_scale=wws[:, g, :],
-                start=g == 0,
-                stop=g == 1,
-            )
+        minus_bq = keep.tile([P, FEATURES], F32, name="minus_bq")
+        bq_piece = keep.tile([P, FEATURES], F32, name="bq_piece")
+        bw_row = keep.tile([P, FEATURES], F32, name="bw_row")
+        alpha_divisor = keep.tile([P, 1], F32, name="alpha_divisor")
+        alpha_recip = keep.tile([P, 1], F32, name="alpha_recip")
+        minus_a_sum = keep.tile([P, 1], F32, name="minus_a_sum")
+        a_slope = keep.tile([P, NEIGHBOURS], F32, name="a_slope")
+        a_rest = keep.tile([P, NEIGHBOURS], F32, name="a_rest")
 
-        def bias():
-            nc.scalar.activation(nb[:], bps[:], ACT.Copy, scale=-1.0)
+        scale(0, separately=True)
+        turn(0)
+        interleave(0)
+        nc.scalar.activation(minus_bq[:], bq_bank[:], ACT.Copy, scale=-1.0)
+        scale(1)
+        nc.gpsimd.tensor_scalar(
+            alpha_divisor[:], alpha_sum[:], 0.0, alpha_sum[:], op0=ALU.is_equal, op1=ALU.add
+        )
+        nc.vector.reciprocal(alpha_recip[:], alpha_divisor[:])
+        nc.gpsimd.tensor_scalar(a_slope[:], alpha_f32[:], alpha_recip[:], SLOPE, op0=ALU.mult, op1=ALU.mult)
+        nc.gpsimd.tensor_scalar(a_rest[:], alpha_f32[:], alpha_recip[:], 1.0 - SLOPE, op0=ALU.mult, op1=ALU.mult)
+        nc.gpsimd.tensor_scalar(minus_a_sum[:], alpha_sum[:], alpha_recip[:], -1.0, op0=ALU.mult, op1=ALU.mult)
+        quantise(0)
+        turn(1)
+        scale(2)
+        multiply(0)
+        interleave(1)
+        nc.scalar.copy(bw_row[:].rearrange("p (i t) -> p i t", t=PACK), plain_order(bw_bank))
+        nc.scalar.activation(bq_piece[:], minus_bq[:], ACT.Copy, scale=minus_a_sum[:])
+        quantise(1)
+        scale(3)
+        turn(2)
+        interleave(2)
 
-        def extras(r):
-            if r == 1:
-                nc.scalar.activation(bsig[:], nb[:], ACT.Copy, scale=nsig[:])
-            if r == 2:
-                nc.vector.quantize_mx(out=hcodes[:].bitcast(FP8X4), scales=hscl[:], in_=hgrp[:])
-            if r == 3:
-                nc.scalar.copy(
-                    bwt[:].rearrange("p (i c) -> p i c", c=4), bwps[:].rearrange("p (c i) -> p i c", c=4)
-                )
-
-        def join(k):
-            t = work.tile([P, 512], F32, name="y", tag="y%d" % (k % 2))
-            nc.vector.scalar_tensor_tensor(
-                planes(t), channels(pt[k]), SLOPE / (1.0 - SLOPE), planes(zt[k]), op0=ALU.mult, op1=ALU.add
-            )
-            zt[k] = t
-
-
-        prod(0, (0, 1))
-        flip(0)
-        gather(0)
-        bias()
-        prod(1)
-        weights()
-        quant(0)
-        flip(1)
-        prod(2)
-        mult(0)
-        gather(1)
-        quant(1)
-        prod(3)
-        flip(2)
-        gather(2)
-
+        node_codes = keep.tile([P, P], U32, name="node_codes", align_bytes=64)
+        node_scales = keep.tile([P, P], U8, name="node_scales", align_bytes=64)
         for r in range(PAIRS):
-            if r + 1 < PAIRS:
-                mult(r + 1)
-            if r == PAIRS - 2:
-                mult2(0, hcodes, hscl)
+            last = r == PAIRS - 1
+            if r + MULT_AHEAD < PAIRS:
+                multiply(r + MULT_AHEAD)
             if r > 0:
-                reduce(r - 1, 0)
-            if r + 3 < PAIRS and True:
-                flip(r + 3)
+                add_first_half(r - 1)
+            if r + TURN_AHEAD < PAIRS:
+                turn(r + TURN_AHEAD)
             if r == 1:
-                bwps = spread(bw32, "bwps")
-            if r == 3:
-                add(bsig)
+                add(bq_piece)
             if r > 0:
-                reduce(r - 1, 1)
+                add_second_half(r - 1)
+
             clip(2 * r + 1)
+            if last:
+                linear(2 * r)
             clip(2 * r)
-            if one_piece(r):
+            if joined(r):
                 join(2 * r + 1)
                 join(2 * r)
-                weigh(2 * r + 1, "scalar")
-                weigh(2 * r, "scalar")
             else:
                 linear(2 * r + 1)
-                linear(2 * r)
-                last = r == PAIRS - 1
-                weigh(2 * r + 1, "vector" if last else "vector")
-                weigh(2 * r, "vector" if last else "scalar")
-            extras(r)
-            if r + 2 < PAIRS:
-                quant(r + 2)
-            if r + 4 < PAIRS:
-                prod(r + 4)
-            if r + 3 < PAIRS:
-                gather(r + 3)
-        reduce(PAIRS - 1, 0)
-        reduce(PAIRS - 1, 1)
+                if not last:
+                    linear(2 * r)
+            weigh(2 * r + 1, by_vector=last or (r % 2 == 1 and not joined(r)))
+            weigh(2 * r, by_vector=last)
 
-        agrp = keep.tile([P, 512], BF16, name="agrp", align_bytes=64)
+            if r == 2:
+                nc.vector.quantize_mx(out=node_codes[:].bitcast(FP8X4), scales=node_scales[:], in_=node_grouped[:])
+            if r + QUANT_AHEAD < PAIRS:
+                quantise(r + QUANT_AHEAD)
+            if r + SCALE_AHEAD < PAIRS:
+                scale(r + SCALE_AHEAD)
+            if r + TURN_AHEAD < PAIRS:
+                interleave(r + TURN_AHEAD)
+        add_first_half(PAIRS - 1)
+        add_second_half(PAIRS - 1)
+
+        h2_bank = single.tile([P, FEATURES], F32, name="h2_bank")
+
+        def multiply_ww(group, group_codes, group_scales):
+            nc.tensor.matmul_mx(
+                out=h2_bank[:],
+                lhsT=group_codes[:].bitcast(FP8X4),
+                lhsT_scale=group_scales[:],
+                rhs=ww_words[:, group, :].bitcast(FP4X4),
+                rhs_scale=ww_scales[:, group, :],
+                start=group == 0,
+                stop=group == 1,
+            )
+
+        multiply_ww(0, node_codes, node_scales)
+        mean_grouped = keep.tile([P, FEATURES], BF16, name="mean_grouped", align_bytes=64)
         nc.scalar.copy(
-            agrp[:].rearrange("p (n t) -> p n t", t=4), acc[:].rearrange("p (t n) -> p n t", t=4)
+            mean_grouped[:].rearrange("p (n t) -> p n t", t=PACK), mean[:].rearrange("p (t n) -> p n t", t=PACK)
         )
-        acodes = keep.tile([P, 128], U32, name="acodes", align_bytes=64)
-        ascl = keep.tile([P, 128], U8, name="ascl", align_bytes=64)
-        nc.vector.quantize_mx(out=acodes[:].bitcast(FP8X4), scales=ascl[:], in_=agrp[:])
-        mult2(1, acodes, ascl)
+        mean_codes = keep.tile([P, P], U32, name="mean_codes", align_bytes=64)
+        mean_scales = keep.tile([P, P], U8, name="mean_scales", align_bytes=64)
+        nc.vector.quantize_mx(out=mean_codes[:].bitcast(FP8X4), scales=mean_scales[:], in_=mean_grouped[:])
+        multiply_ww(1, mean_codes, mean_scales)
 
-        t2 = keep.tile([P, 512], F32, name="t2")
-        y2 = keep.tile([P, 512 + 1], F32, name="y2")
-        sq = keep.tile([P, 512 + 1], F32, name="sq")
-        res = [keep.tile([P, 256], F32, name="res%d" % i) for i in range(2)]
-        ss = [keep.tile([P, 1], F32, name="ss%d" % i) for i in range(2)]
-        nrec = keep.tile([P, 1], F32, name="nrec")
-        nc.gpsimd.memset(y2[:, 512:], TINY)
-        halves = (slice(0, 256), slice(256, 512))
-        for h in halves:
-            nc.vector.tensor_tensor(t2[:, h], p2[:, h], bwt[:, h], op=ALU.add)
-        for h in halves:
-            nc.vector.scalar_tensor_tensor(y2[:, h], t2[:, h], SLOPE, t2[:, h], op0=ALU.mult, op1=ALU.max)
-        for i, h in enumerate((slice(0, 256), slice(256, 513))):
-            nc.scalar.activation(sq[:, h], y2[:, h], ACT.Square, accum_out=ss[i][:])
-        nc.scalar.activation(nrec[:], ss[0][:], ACT.Abs_reciprocal_sqrt, bias=ss[1][:])
-        nc.vector.tensor_scalar(res[0][:], y2[:, halves[0]], nrec[:], None, op0=ALU.mult)
-        nc.scalar.activation(res[1][:], y2[:, halves[1]], ACT.Copy, scale=nrec[:])
-        nc.sync.dma_start(out=out[:, halves[0]], in_=res[0][:])
-        nc.scalar.dma_start(out=out[:, halves[1]], in_=res[1][:])
+        biased = keep.tile([P, FEATURES], F32, name="biased")
+        h2 = keep.tile([P, FEATURES + 1], F32, name="h2")
+        squares = keep.tile([P, FEATURES + 1], F32, name="squares")
+        result = [keep.tile([P, FEATURES // 2], F32, name="result%d" % i) for i in range(2)]
+        square_sum = [keep.tile([P, 1], F32, name="square_sum%d" % i) for i in range(2)]
+        norm_recip = keep.tile([P, 1], F32, name="norm_recip")
+        nc.gpsimd.memset(h2[:, FEATURES:], TINY)
+        halves = (slice(0, FEATURES // 2), slice(FEATURES // 2, FEATURES))
+        for half in halves:
+            nc.vector.tensor_tensor(biased[:, half], h2_bank[:, half], bw_row[:, half], op=ALU.add)
+        for half in halves:
+            nc.vector.scalar_tensor_tensor(
+                h2[:, half], biased[:, half], SLOPE, biased[:, half], op0=ALU.mult, op1=ALU.max
+            )
+        for i, columns in enumerate((halves[0], slice(FEATURES // 2, FEATURES + 1))):
+            nc.scalar.activation(squares[:, columns], h2[:, columns], ACT.Square, accum_out=square_sum[i][:])
+        nc.scalar.activation(norm_recip[:], square_sum[0][:], ACT.Abs_reciprocal_sqrt, bias=square_sum[1][:])
+        nc.vector.tensor_scalar(result[0][:], h2[:, halves[0]], norm_recip[:], None, op0=ALU.mult)
+        nc.scalar.activation(result[1][:], h2[:, halves[1]], ACT.Copy, scale=norm_recip[:])
+        nc.sync.dma_start(out=out[:, halves[0]], in_=result[0][:])
+        nc.scalar.dma_start(out=out[:, halves[1]], in_=result[1][:])

from contextlib import ExitStack

import concourse.mybir as mybir
from concourse.masks import make_identity

F32 = mybir.dt.float32
BF16 = mybir.dt.bfloat16
I32 = mybir.dt.int32
U32 = mybir.dt.uint32
U8 = mybir.dt.uint8
FP8 = mybir.dt.float8_e4m3fn
FP8X4 = mybir.dt.float8_e4m3fn_x4
FP4X4 = mybir.dt.float4_e2m1fn_x4
ALU = mybir.AluOpType
ACT = mybir.ActivationFunctionType

P = 128
FEATURES = 512
PACK = 4
NEIGHBOURS = 32
PAIRS = NEIGHBOURS // 2
SLOPE = 0.01
TINY = 2.0**-60

LOADS = (2, 2, 4, 8, 8, 8)

SCALE_AHEAD = 4
TURN_AHEAD = 3
QUANT_AHEAD = 2
MULT_AHEAD = 1

FLOPS = 2 * P * NEIGHBOURS * FEATURES * FEATURES + 2 * P * (2 * FEATURES) * FEATURES


def turned_by_matmul(j):
    return 2 < j < 15 and j % 3 != 0


def joined(j):
    return j == PAIRS - 2


def tile_pinsageconv_w4_kernel(
    tc, h_node, h_ngbrs_bytes, h_ngbrs_scale, alpha, Wq_words, Wq_scales, bq, Ww_words, Ww_scales, bw, out
):
    nc = tc.nc
    with ExitStack() as ctx:
        keep = ctx.enter_context(tc.tile_pool(name="keep", bufs=1))
        work = ctx.enter_context(tc.tile_pool(name="work", bufs=4))
        products = ctx.enter_context(tc.psum_pool(name="products", bufs=4))
        turned_pool = ctx.enter_context(tc.psum_pool(name="turned_pool", bufs=2))
        single = ctx.enter_context(tc.psum_pool(name="single", bufs=1))
        ctx.enter_context(tc.manual_schedule())

        ident = keep.tile([P, P], F32, name="ident")
        ident_bf = keep.tile([P, P], BF16, name="ident_bf")
        make_identity(nc, ident[:])
        nc.gpsimd.tensor_copy(ident_bf[:], ident[:])

        wq_scales = keep.tile([P, FEATURES], U8, name="wq_scales", align_bytes=64)
        ww_scales = keep.tile([P, 2, FEATURES], U8, name="ww_scales", align_bytes=64)
        nc.gpsimd.memset(wq_scales[:].bitcast(I32), 0)
        nc.gpsimd.memset(ww_scales[:].rearrange("p g n -> p (g n)").bitcast(I32), 0)

        x_scale = keep.tile([P, PACK], F32, name="x_scale")
        alpha_bf = keep.tile([P, NEIGHBOURS], BF16, name="alpha_bf")
        bq_bf = keep.tile([P, PACK], BF16, name="bq_bf")
        node = keep.tile([P, FEATURES], BF16, name="node")
        bw_bf = keep.tile([P, PACK], BF16, name="bw_bf")
        nc.scalar.dma_start(out=x_scale[:], in_=h_ngbrs_scale.rearrange("a b (p t) -> p (a b t)", t=PACK))
        nc.scalar.dma_start(out=alpha_bf[:], in_=alpha.rearrange("n k o -> n (k o)"))
        nc.scalar.dma_start(out=bq_bf[:], in_=bq.rearrange("(p t) -> p t", t=PACK))
        nc.scalar.dma_start(out=node[:], in_=h_node)
        nc.scalar.dma_start(out=bw_bf[:], in_=bw.rearrange("(p t) -> p t", t=PACK))

        wq_words = keep.tile([P, 2 * FEATURES], U8, name="wq_words", align_bytes=64)
        ww_words = keep.tile([P, 2, 2 * FEATURES], U8, name="ww_words", align_bytes=64)
        token_bytes = []
        for i, count in enumerate(LOADS):
            first_k = len(token_bytes)
            loaded = keep.tile([P, count * FEATURES], U8, name="loaded%d" % i, align_bytes=64)
            nc.sync.dma_start(
                out=loaded[:], in_=h_ngbrs_bytes[:, first_k : first_k + count, :].rearrange("n k f -> n (k f)")
            )
            token_bytes.extend([(loaded, place) for place in range(count)])
            if i == 0:
                nc.sync.dma_start(out=wq_words[:].bitcast(I32), in_=Wq_words[0].bitcast(I32))
                for q in range(4):
                    nc.sync.dma_start(
                        out=wq_scales[32 * q : 32 * q + 4, :].bitcast(I32),
                        in_=Wq_scales[0, 4 * q : 4 * q + 4, :].bitcast(I32),
                    )
        nc.sync.dma_start(out=ww_words[:].bitcast(I32), in_=Ww_words.rearrange("g p n -> p g n").bitcast(I32))
        for q in range(4):
            nc.sync.dma_start(
                out=ww_scales[32 * q : 32 * q + 4, :, :].bitcast(I32),
                in_=Ww_scales[:, 4 * q : 4 * q + 4, :].rearrange("g q n -> q g n").bitcast(I32),
            )

        table = keep.tile([P, 1], F32, name="table")
        nc.vector.memset(table[:], 1.0)
        nc.scalar.activation(table[:], table[:], ACT.Abs_reciprocal_sqrt)

        def spread(column_tile, name):
            bank = products.tile([P, FEATURES], F32, name=name, tag="product")
            for t in range(PACK):
                nc.tensor.transpose(
                    bank[:, P * t : P * (t + 1)], column_tile[:, t : t + 1].to_broadcast([P, P]), ident[:]
                )
            return bank

        def plain_order(bank):
            return bank[:].rearrange("p (t i) -> p i t", t=PACK)

        bq_f32 = keep.tile([P, PACK], F32, name="bq_f32")
        bw_f32 = keep.tile([P, PACK], F32, name="bw_f32")
        nc.gpsimd.tensor_copy(bq_f32[:], bq_bf[:])
        nc.gpsimd.tensor_copy(bw_f32[:], bw_bf[:])

        scale_row = keep.tile([P, 2, FEATURES], F32, name="scale_row")
        alpha_f32 = keep.tile([P, NEIGHBOURS], F32, name="alpha_f32")
        alpha_sum = keep.tile([P, 1], F32, name="alpha_sum")
        scale_bank = spread(x_scale, "scale_bank")
        nc.scalar.copy(scale_row[:, 0, :].rearrange("p (i t) -> p i t", t=PACK), plain_order(scale_bank))
        nc.scalar.activation(alpha_f32[:], alpha_bf[:], ACT.Copy, accum_out=alpha_sum[:])
        nc.scalar.copy(scale_row[:, 1, :].rearrange("p (i t) -> p i t", t=PACK), plain_order(scale_bank))

        node_bank = products.tile([P, FEATURES], F32, name="node_bank", tag="product")
        node_words = node[:].bitcast(F32)
        for u in range(2):
            nc.tensor.transpose(node_bank[:, P * u : P * (u + 1)], node_words[:, u : FEATURES // 2 : 2], ident[:])
        node_grouped = keep.tile([P, FEATURES], BF16, name="node_grouped", align_bytes=64)
        nc.scalar.copy(
            node_grouped[:].bitcast(F32).rearrange("p (n u) -> p n u", u=2),
            node_bank[:, : FEATURES // 2].rearrange("p (u n) -> p n u", u=2),
        )
        bq_bank = spread(bq_f32, "bq_bank")
        bw_bank = spread(bw_f32, "bw_bank")

        scaled, turned, grouped, codes, code_scales = {}, {}, {}, {}, {}
        product, clipped, linear_piece, weighed_piece = {}, {}, {}, {}

        def scale(j, separately=False):
            scaled[j] = work.tile([P, 2 * FEATURES], BF16, name="scaled", tag="scaled", align_bytes=64)
            loaded, place = token_bytes[2 * j]
            for start, stop in ((0, 1), (1, 2)) if separately else ((0, 2),):
                nc.vector.tensor_tensor(
                    scaled[j][:, start * FEATURES : stop * FEATURES],
                    loaded[:, (place + start) * FEATURES : (place + stop) * FEATURES].bitcast(FP8),
                    scale_row[:, 0 : stop - start, :].rearrange("p x f -> p (x f)"),
                    op=ALU.mult,
                )

        def turn(j):
            turned[j] = turned_pool.tile([P, 2 * FEATURES // 2], F32, name="turned", tag="turned")
            words = scaled[j][:].bitcast(F32)
            half = FEATURES // 2
            for x in range(2):
                if x == 0 and turned_by_matmul(j):
                    for t in range(PACK):
                        nc.tensor.matmul(
                            turned[j][:].bitcast(BF16)[:, P * t : P * (t + 1)],
                            lhsT=scaled[j][:, t:FEATURES:PACK],
                            rhs=ident_bf[:],
                            start=True,
                            stop=True,
                        )
                else:
                    for u in range(2):
                        place = half * x + P * u
                        nc.tensor.transpose(
                            turned[j][:, place : place + P], words[:, half * x + u : half * (x + 1) : 2], ident[:]
                        )

        def interleave(j):
            grouped[j] = work.tile([P, 2 * FEATURES], BF16, name="grouped", tag="grouped", align_bytes=64)
            half = FEATURES // 2
            if turned_by_matmul(j):
                nc.scalar.copy(
                    grouped[j][:, :FEATURES].rearrange("p (n t) -> p n t", t=PACK),
                    turned[j][:].bitcast(BF16)[:, :FEATURES].rearrange("p (t n) -> p n t", t=PACK),
                )
                nc.scalar.copy(
                    grouped[j][:, FEATURES:].bitcast(F32).rearrange("p (n u) -> p n u", u=2),
                    turned[j][:, half:].rearrange("p (u n) -> p n u", u=2),
                )
            else:
                nc.scalar.copy(
                    grouped[j][:].bitcast(F32).rearrange("p (x n u) -> p x n u", x=2, u=2),
                    turned[j][:].rearrange("p (x u n) -> p x n u", x=2, u=2),
                )

        def quantise(j):
            codes[j] = work.tile([P, 2 * P], U32, name="codes", tag="codes", align_bytes=64)
            code_scales[j] = work.tile([P, 2 * P], U8, name="code_scales", tag="code_scales", align_bytes=64)
            nc.vector.quantize_mx(out=codes[j][:].bitcast(FP8X4), scales=code_scales[j][:], in_=grouped[j][:])

        def multiply(j):
            for x in (1, 0):
                bank = products.tile([P, FEATURES], F32, name="product", tag="product")
                product[2 * j + x] = bank
                nodes = slice(P * x, P * (x + 1))
                nc.tensor.matmul_mx(
                    out=bank[:],
                    lhsT=codes[j][:, nodes].bitcast(FP8X4),
                    lhsT_scale=code_scales[j][:, nodes],
                    rhs=wq_words[:].bitcast(FP4X4),
                    rhs_scale=wq_scales[:],
                    start=True,
                    stop=True,
                )

        def channels(bank):
            return bank[:].rearrange("n (p t) -> n t p", t=PACK)

        def planes(piece):
            return piece[:].rearrange("n (t p) -> n t p", t=PACK)

        def clip(k):
            clipped[k] = work.tile([P, FEATURES], F32, name="clipped", tag="clipped%d" % (k % 2))
            nc.vector.tensor_tensor(planes(clipped[k]), channels(product[k]), planes(minus_bq), op=ALU.max)

        def linear(k):
            linear_piece[k] = work.tile([P, FEATURES], F32, name="linear_piece", tag="linear%d" % (k % 2))
            nc.scalar.activation(planes(linear_piece[k]), channels(product[k]), ACT.Copy, scale=a_slope[:, k : k + 1])

        def join(k):
            both = work.tile([P, FEATURES], F32, name="both", tag="both%d" % (k % 2))
            nc.vector.scalar_tensor_tensor(
                planes(both), channels(product[k]), SLOPE / (1.0 - SLOPE), planes(clipped[k]), op0=ALU.mult, op1=ALU.add
            )
            clipped[k] = both

        def weigh(k, by_vector=False):
            weighed_piece[k] = work.tile([P, FEATURES], F32, name="weighed_piece", tag="weighed%d" % (k % 2))
            factor = a_rest[:, k : k + 1]
            if by_vector:
                nc.vector.tensor_scalar(weighed_piece[k][:], clipped[k][:], factor, None, op0=ALU.mult)
            else:
                nc.scalar.activation(weighed_piece[k][:], clipped[k][:], ACT.Copy, scale=factor)

        mean = single.tile([P, FEATURES], F32, name="mean")

        def add(piece, first=False, last=False):
            for t in range(PACK):
                nc.tensor.matmul(
                    mean[:, P * t : P * (t + 1)],
                    lhsT=piece[:, P * t : P * (t + 1)],
                    rhs=ident[:],
                    start=first and t == 0,
                    stop=last and t == PACK - 1,
                    is_transpose=True,
                )

        def add_first_half(j):
            if joined(j):
                add(weighed_piece[2 * j + 1])
            else:
                add(linear_piece[2 * j + 1], first=j == 0)
                add(linear_piece[2 * j])

        def add_second_half(j):
            if not joined(j):
                add(weighed_piece[2 * j + 1])
            add(weighed_piece[2 * j], last=j == PAIRS - 1)

        minus_bq = keep.tile([P, FEATURES], F32, name="minus_bq")
        bq_piece = keep.tile([P, FEATURES], F32, name="bq_piece")
        bw_row = keep.tile([P, FEATURES], F32, name="bw_row")
        alpha_divisor = keep.tile([P, 1], F32, name="alpha_divisor")
        alpha_recip = keep.tile([P, 1], F32, name="alpha_recip")
        minus_a_sum = keep.tile([P, 1], F32, name="minus_a_sum")
        a_slope = keep.tile([P, NEIGHBOURS], F32, name="a_slope")
        a_rest = keep.tile([P, NEIGHBOURS], F32, name="a_rest")

        scale(0, separately=True)
        turn(0)
        interleave(0)
        nc.scalar.activation(minus_bq[:], bq_bank[:], ACT.Copy, scale=-1.0)
        scale(1)
        nc.gpsimd.tensor_scalar(
            alpha_divisor[:], alpha_sum[:], 0.0, alpha_sum[:], op0=ALU.is_equal, op1=ALU.add
        )
        nc.vector.reciprocal(alpha_recip[:], alpha_divisor[:])
        nc.gpsimd.tensor_scalar(a_slope[:], alpha_f32[:], alpha_recip[:], SLOPE, op0=ALU.mult, op1=ALU.mult)
        nc.gpsimd.tensor_scalar(a_rest[:], alpha_f32[:], alpha_recip[:], 1.0 - SLOPE, op0=ALU.mult, op1=ALU.mult)
        nc.gpsimd.tensor_scalar(minus_a_sum[:], alpha_sum[:], alpha_recip[:], -1.0, op0=ALU.mult, op1=ALU.mult)
        quantise(0)
        turn(1)
        scale(2)
        multiply(0)
        interleave(1)
        nc.scalar.copy(bw_row[:].rearrange("p (i t) -> p i t", t=PACK), plain_order(bw_bank))
        nc.scalar.activation(bq_piece[:], minus_bq[:], ACT.Copy, scale=minus_a_sum[:])
        quantise(1)
        scale(3)
        turn(2)
        interleave(2)

        node_codes = keep.tile([P, P], U32, name="node_codes", align_bytes=64)
        node_scales = keep.tile([P, P], U8, name="node_scales", align_bytes=64)
        for r in range(PAIRS):
            last = r == PAIRS - 1
            if r + MULT_AHEAD < PAIRS:
                multiply(r + MULT_AHEAD)
            if r > 0:
                add_first_half(r - 1)
            if r + TURN_AHEAD < PAIRS:
                turn(r + TURN_AHEAD)
            if r == 1:
                add(bq_piece)
            if r > 0:
                add_second_half(r - 1)

            clip(2 * r + 1)
            if last:
                linear(2 * r)
            clip(2 * r)
            if joined(r):
                join(2 * r + 1)
                join(2 * r)
            else:
                linear(2 * r + 1)
                if not last:
                    linear(2 * r)
            weigh(2 * r + 1, by_vector=last or (r % 2 == 1 and not joined(r)))
            weigh(2 * r, by_vector=last)

            if r == 2:
                nc.vector.quantize_mx(out=node_codes[:].bitcast(FP8X4), scales=node_scales[:], in_=node_grouped[:])
            if r + QUANT_AHEAD < PAIRS:
                quantise(r + QUANT_AHEAD)
            if r + SCALE_AHEAD < PAIRS:
                scale(r + SCALE_AHEAD)
            if r + TURN_AHEAD < PAIRS:
                interleave(r + TURN_AHEAD)
        add_first_half(PAIRS - 1)
        add_second_half(PAIRS - 1)

        h2_bank = single.tile([P, FEATURES], F32, name="h2_bank")

        def multiply_ww(group, group_codes, group_scales):
            nc.tensor.matmul_mx(
                out=h2_bank[:],
                lhsT=group_codes[:].bitcast(FP8X4),
                lhsT_scale=group_scales[:],
                rhs=ww_words[:, group, :].bitcast(FP4X4),
                rhs_scale=ww_scales[:, group, :],
                start=group == 0,
                stop=group == 1,
            )

        multiply_ww(0, node_codes, node_scales)
        mean_grouped = keep.tile([P, FEATURES], BF16, name="mean_grouped", align_bytes=64)
        nc.scalar.copy(
            mean_grouped[:].rearrange("p (n t) -> p n t", t=PACK), mean[:].rearrange("p (t n) -> p n t", t=PACK)
        )
        mean_codes = keep.tile([P, P], U32, name="mean_codes", align_bytes=64)
        mean_scales = keep.tile([P, P], U8, name="mean_scales", align_bytes=64)
        nc.vector.quantize_mx(out=mean_codes[:].bitcast(FP8X4), scales=mean_scales[:], in_=mean_grouped[:])
        multiply_ww(1, mean_codes, mean_scales)

        biased = keep.tile([P, FEATURES], F32, name="biased")
        h2 = keep.tile([P, FEATURES + 1], F32, name="h2")
        squares = keep.tile([P, FEATURES + 1], F32, name="squares")
        result = [keep.tile([P, FEATURES // 2], F32, name="result%d" % i) for i in range(2)]
        square_sum = [keep.tile([P, 1], F32, name="square_sum%d" % i) for i in range(2)]
        norm_recip = keep.tile([P, 1], F32, name="norm_recip")
        nc.gpsimd.memset(h2[:, FEATURES:], TINY)
        halves = (slice(0, FEATURES // 2), slice(FEATURES // 2, FEATURES))
        for half in halves:
            nc.vector.tensor_tensor(biased[:, half], h2_bank[:, half], bw_row[:, half], op=ALU.add)
        for half in halves:
            nc.vector.scalar_tensor_tensor(
                h2[:, half], biased[:, half], SLOPE, biased[:, half], op0=ALU.mult, op1=ALU.max
            )
        for i, columns in enumerate((halves[0], slice(FEATURES // 2, FEATURES + 1))):
            nc.scalar.activation(squares[:, columns], h2[:, columns], ACT.Square, accum_out=square_sum[i][:])
        nc.scalar.activation(norm_recip[:], square_sum[0][:], ACT.Abs_reciprocal_sqrt, bias=square_sum[1][:])
        nc.vector.tensor_scalar(result[0][:], h2[:, halves[0]], norm_recip[:], None, op0=ALU.mult)
        nc.scalar.activation(result[1][:], h2[:, halves[1]], ACT.Copy, scale=norm_recip[:])
        nc.sync.dma_start(out=out[:, halves[0]], in_=result[0][:])
        nc.scalar.dma_start(out=out[:, halves[1]], in_=result[1][:])
